import numpy as np
import ml_dtypes


def mxq(x, axis, fmt="e4m3"):
    dtype, down = {"e4m3": (ml_dtypes.float8_e4m3fn, 7), "e5m2": (ml_dtypes.float8_e5m2, 14)}[fmt]
    v = np.moveaxis(np.asarray(x, np.float32).astype(ml_dtypes.bfloat16).astype(np.float64), axis, -1)
    blocks = v.reshape(v.shape[:-1] + (-1, 32))
    amax = np.abs(blocks).max(-1, keepdims=True)
    byte = np.maximum(np.where(amax > 0, np.frexp(amax)[1] - 1 + 127, 0) - down, 1)
    scale = np.exp2(byte - 127.0)
    codes = (blocks / scale).astype(np.float32).astype(dtype).astype(np.float64)
    return np.moveaxis((codes * scale).reshape(v.shape), -1, axis)


WIDE = False


def mx_kscale(k):
    if not WIDE:
        return np.ones(k)
    levels = np.array([10, -10, 5, -5, 0])
    if k % 512:
        return np.exp2(np.random.permutation(np.resize(levels, k // 32))).repeat(32)
    a = np.empty((k // 512, 16))
    for p in range(k // 512):
        a[p, :8] = np.random.permutation(np.resize(levels, 8))
        for g in range(8):
            far = levels[np.abs(levels - a[p, g]) >= 10]
            a[p, g + 8] = far[np.random.randint(len(far))]
    return np.exp2(a.ravel()).repeat(32)


BF16 = ml_dtypes.bfloat16


def bf(x):
    return np.asarray(x, np.float32).astype(BF16)


def f64(x):
    return np.asarray(x).astype(np.float64)


B, L, H, G, DEPTH = 64, 64, 1024, 256, 3
EPS = 1e-5


def layernorm(v, g, b):
    mu = v.mean(-1, keepdims=True)
    var = np.square(v - mu).mean(-1, keepdims=True)
    return (v - mu) / np.sqrt(var + EPS) * g + b


def setup_inputs():
    s, t = mx_kscale(H), mx_kscale(H)
    return {"x_nodes": bf(np.random.standard_normal((B, L, H)) * s),
            "w1": bf(np.random.standard_normal((H, H)) / np.sqrt(H) / s[:, None]),
            "b1": bf(np.random.standard_normal(H) * 0.3),
            "gamma": bf((1.0 + 0.1 * np.random.standard_normal(H)) * t),
            "beta": bf(0.2 * np.random.standard_normal(H) * t),
            "w2": bf(np.random.standard_normal((H, G)) / np.sqrt(H) / t[:, None]),
            "b2": bf(np.random.standard_normal(G) * 0.3)}


def reference(x_nodes, w1, b1, gamma, beta, w2, b2):
    h = (mxq(f64(x_nodes), 2, "e4m3") @ mxq(f64(w1), 0, "e4m3")) + f64(b1)
    r = np.maximum(layernorm(h, f64(gamma), f64(beta)), 0.0)
    x1 = (mxq(r, 2, "e4m3") @ mxq(f64(w2), 0, "e4m3")) + f64(b2)
    x2 = np.broadcast_to(x1.max(axis=1, keepdims=True), x1.shape)
    return np.concatenate([x1, x2], axis=2)

@@ -1,0 +1,446 @@
+from contextlib import ExitStack
+
+import concourse.mybir as mybir
+from concourse.masks import make_identity
+
+F32 = mybir.dt.float32
+BF16 = mybir.dt.bfloat16
+U32 = mybir.dt.uint32
+U8 = mybir.dt.uint8
+FP8X4 = mybir.dt.float8_e4m3fn_x4
+ALU = mybir.AluOpType
+ACT = mybir.ActivationFunctionType
+AXIS = mybir.AxisListType
+
+P = 128
+PACK = 4
+K_PASS = P * PACK
+BANK = 512
+
+TOKENS = 64 * 64
+NODES = 64
+HIDDEN = 1024
+FEATURES = 256
+PASSES = HIDDEN // K_PASS
+SLICES = HIDDEN // P
+GROUP = 4
+GROUP_TOKENS = GROUP * P
+N_GROUPS = TOKENS // GROUP_TOKENS
+GROUP_LINES = GROUP_TOKENS // NODES
+COPIES = P // GROUP_LINES
+EPS = 1e-5
+
+FLOPS = 2 * TOKENS * HIDDEN * (HIDDEN + FEATURES)
+
+
+N_TILES = TOKENS // P
+HALVES = HIDDEN // BANK
+PAIR_LINES = 2 * P // NODES
+
+X_AHEAD = 8
+RELU_LAG = 6
+QUANT_LAG = 8
+LAYER2_LAG = 11
+POOL_LAG = LAYER2_LAG + 2
+STORE_LAG = POOL_LAG + 3
+N_STEPS = N_TILES - GROUP + STORE_LAG + 1
+SCALAR_SHARE = 4
+
+
+def due(step, lag, period):
+    if step < lag or (step - lag) % period != 0:
+        return -1
+    return (step - lag) // period
+
+
+def regroup(copy, grouped, planes):
+    copy(
+        out=grouped.rearrange("p (n i) t -> p n t i", i=4),
+        in_=planes.rearrange("p t (n i) -> p n t i", i=4),
+    )
+
+
+def tile_sub_graph_pa_t_kernel(tc, x_nodes, w1, b1, gamma, beta, w2, b2, out):
+    nc = tc.nc
+    x_rows = x_nodes.flatten_outer_dims()
+    out_rows = out.flatten_outer_dims()
+
+    with ExitStack() as ctx:
+        consts = ctx.enter_context(tc.tile_pool(name="consts", bufs=1))
+        stage = ctx.enter_context(tc.tile_pool(name="stage", bufs=2))
+        psum = ctx.enter_context(tc.psum_pool(name="psum", bufs=1))
+
+        x_tiles, x_words, x_quantised = {}, {}, {}
+        normed, row_sums, minus_mean, inv_std = {}, {}, {}, {}
+        r_planes, r_grouped, r_quantised = {}, {}, {}
+        x1_tiles, line_max, repeated = {}, {}, {}
+
+        def load_x(i):
+            if i >= N_TILES:
+                return
+            x_sb = stage.tile([P, HIDDEN], BF16, tag="x_sb", bufs=X_AHEAD + 2)
+            nc.sync.dma_start(out=x_sb[:], in_=x_rows[i * P : (i + 1) * P, :])
+            x_tiles[i] = x_sb
+
+        w1_planes = consts.tile([P, PASSES * PACK, HIDDEN], BF16)
+        w1_passes = w1.rearrange("(c p t) n -> c p t n", c=PASSES, p=P, t=PACK)
+
+        def load_w1_half(half):
+            cols = slice(half * BANK, (half + 1) * BANK)
+            for c in range(PASSES):
+                nc.sync.dma_start(
+                    out=w1_planes[:, PACK * c : PACK * (c + 1), cols], in_=w1_passes[c][:, :, cols]
+                )
+
+        affine_rows = consts.tile([P, K_PASS], BF16)
+        nc.vector.memset(affine_rows[:], 0.0)
+        eps = consts.tile([P, 1], F32)
+        nc.vector.memset(eps[:], EPS)
+        ident = consts.tile([P, P], F32)
+        make_identity(nc, ident[:])
+
+        nc.scalar.dma_start(out=affine_rows[0:PASSES, :], in_=gamma.rearrange("(c n) -> c n", c=PASSES))
+        nc.scalar.dma_start(
+            out=affine_rows[PASSES : 2 * PASSES, :], in_=beta.rearrange("(c n) -> c n", c=PASSES)
+        )
+        bias_rows = consts.tile([P, HIDDEN + FEATURES], BF16)
+        nc.vector.memset(bias_rows[:], 0.0)
+        ones = consts.tile([P, P], BF16)
+        nc.vector.memset(ones[:], 1.0)
+        nc.scalar.dma_start(out=bias_rows[0:1, 0:HIDDEN], in_=b1.rearrange("(o n) -> o n", o=1))
+        nc.scalar.dma_start(out=bias_rows[0:1, HIDDEN:], in_=b2.rearrange("(o n) -> o n", o=1))
+
+        load_x(0)
+        load_w1_half(0)
+        load_x(1)
+        load_w1_half(1)
+        w2_planes = consts.tile([P, PASSES * PACK, FEATURES], BF16)
+        for c in range(PASSES):
+            nc.sync.dma_start(
+                out=w2_planes[:, PACK * c : PACK * (c + 1), :],
+                in_=w2[c * K_PASS : (c + 1) * K_PASS, :].rearrange("(p t) n -> p t n", t=PACK),
+            )
+        for i in range(2, X_AHEAD):
+            load_x(i)
+
+        def transpose_x(i):
+            if i >= N_TILES:
+                return
+            words = x_tiles[i][:].bitcast(F32)
+            xT_ps = psum.tile([P, PASSES, 2, P], F32, tag="xT", bufs=2)
+            for c in range(PASSES):
+                for u in range(2):
+                    nc.tensor.transpose(
+                        out=xT_ps[:, c, u, :],
+                        in_=words[:, 2 * P * c + u : 2 * P * (c + 1) : 2],
+                        identity=ident[:],
+                    )
+            x_grouped = stage.tile([P, PASSES, P, 2], F32, tag="x_grouped", bufs=3, align_bytes=64)
+            nc.scalar.copy(out=x_grouped[:], in_=xT_ps[:].rearrange("q c u r -> q c r u"))
+            x_words[i] = x_grouped
+
+        def quantise_x(i):
+            if i >= N_TILES:
+                return
+            x_codes = stage.tile([P, PASSES, P], U32, tag="x_codes", bufs=3, align_bytes=64)
+            x_scales = stage.tile([P, PASSES, P], U8, tag="x_scales", bufs=3, align_bytes=64)
+            nc.vector.quantize_mx(
+                out=x_codes[:].rearrange("q c r -> q (c r)").bitcast(FP8X4),
+                scales=x_scales[:].rearrange("q c r -> q (c r)"),
+                in_=x_words[i][:].rearrange("q c r u -> q (c r u)").bitcast(BF16),
+            )
+            x_quantised[i] = (x_codes, x_scales)
+
+        def first_layer(i):
+            if i >= N_TILES:
+                return
+            x_codes, x_scales = x_quantised[i]
+            biased = stage.tile([P, HIDDEN], F32, tag="normed", bufs=12)
+            sums = stage.tile([P, HALVES], F32, tag="sums", bufs=4)
+            for half in range(HALVES):
+                cols = slice(half * BANK, (half + 1) * BANK)
+                h_ps = psum.tile([P, BANK], F32, tag="h", bufs=2)
+                for c in range(PASSES):
+                    nc.tensor.matmul_mx(
+                        out=h_ps[:],
+                        lhsT=x_codes[:, c, :].bitcast(FP8X4),
+                        lhsT_scale=x_scales[:, c, :],
+                        rhs=w1_codes[:, c, cols].bitcast(FP8X4),
+                        rhs_scale=w1_scales[:, c, cols],
+                        start=(c == 0),
+                        stop=(c == PASSES - 1),
+                    )
+                nc.vector.scalar_tensor_tensor(
+                    out=biased[:, cols].rearrange("r (t p) -> r t p", t=PACK),
+                    in0=h_ps[:].rearrange("r (p t) -> r t p", t=PACK),
+                    scalar=1.0,
+                    in1=b1_all[:, cols].rearrange("r (t p) -> r t p", t=PACK),
+                    op0=ALU.mult,
+                    op1=ALU.add,
+                    accum_out=sums[:, half : half + 1],
+                )
+            normed[i] = biased
+            row_sums[i] = sums
+
+        def deviation(i):
+            if not 0 <= i < N_TILES:
+                return
+            scaled_sums = stage.tile([P, HALVES], F32, tag="scaled_sums", bufs=2)
+            negated = stage.tile([P, 1], F32, tag="minus_mean", bufs=6)
+            nc.scalar.activation(
+                out=scaled_sums[:],
+                in_=row_sums[i][:],
+                func=ACT.Identity,
+                scale=-1.0 / HIDDEN,
+                accum_out=negated[:, 0:1],
+            )
+            minus_mean[i] = negated
+            squares = stage.tile([P, HIDDEN], BF16, tag="squares", bufs=2)
+            sum_sq = stage.tile([P, 1], F32, tag="sum_sq", bufs=3)
+            nc.scalar.activation(
+                out=squares[:],
+                in_=normed[i][:],
+                func=ACT.Square,
+                bias=minus_mean[i][:, 0:1],
+                scale=1.0,
+                accum_out=sum_sq[:, 0:1],
+            )
+            inverse = stage.tile([P, 1], F32, tag="inv_std", bufs=4)
+            nc.scalar.activation(
+                out=inverse[:],
+                in_=sum_sq[:],
+                func=ACT.Abs_reciprocal_sqrt,
+                bias=eps[:, 0:1],
+                scale=1.0 / HIDDEN,
+            )
+            inv_std[i] = inverse
+
+        def normalise(i):
+            if not 0 <= i < N_TILES:
+                return
+            if i % SCALAR_SHARE == 0:
+                shift = stage.tile([P, 1], F32, tag="shift", bufs=2)
+                nc.scalar.mul(out=shift[:], in_=minus_mean[i][:], mul=inv_std[i][:, 0:1])
+                nc.scalar.activation(
+                    out=normed[i][:],
+                    in_=normed[i][:],
+                    func=ACT.Identity,
+                    bias=shift[:, 0:1],
+                    scale=inv_std[i][:, 0:1],
+                )
+                return
+            nc.vector.tensor_scalar(
+                out=normed[i][:],
+                in0=normed[i][:],
+                scalar1=minus_mean[i][:, 0:1],
+                scalar2=inv_std[i][:, 0:1],
+                op0=ALU.add,
+                op1=ALU.mult,
+            )
+
+        def relu_slice(index):
+            if not 0 <= index < N_GROUPS * SLICES:
+                return
+            group, s = divmod(index, SLICES)
+            if s == 0:
+                planes = stage.tile([P, SLICES, GROUP_TOKENS], BF16, tag="r_planes", bufs=2)
+                r_planes[group] = planes
+            normedT_ps = psum.tile([P, GROUP_TOKENS], F32, tag="normedT", bufs=2)
+            for g in range(GROUP):
+                nc.tensor.transpose(
+                    out=normedT_ps[:, g * P : (g + 1) * P],
+                    in_=normed[group * GROUP + g][:, s * P : (s + 1) * P],
+                    identity=ident[:],
+                )
+            nc.scalar.activation(
+                out=r_planes[group][:, s, :],
+                in_=normedT_ps[:],
+                func=ACT.Relu,
+                bias=affine_cols[:, s % PACK, PASSES + s // PACK : PASSES + s // PACK + 1],
+                scale=affine_cols[:, s % PACK, s // PACK : s // PACK + 1],
+            )
+
+        def regroup_r(index):
+            if not 0 <= index < N_GROUPS * PASSES:
+                return
+            group, c = divmod(index, PASSES)
+            grouped = stage.tile([P, GROUP_TOKENS, PACK], BF16, tag="r_grouped", bufs=2, align_bytes=64)
+            regroup(nc.vector.tensor_copy, grouped[:], r_planes[group][:, PACK * c : PACK * (c + 1), :])
+            r_grouped[index] = grouped
+
+        def quantise_r(index):
+            if not 0 <= index < N_GROUPS * PASSES:
+                return
+            group, c = divmod(index, PASSES)
+            if c == 0:
+                codes = stage.tile([P, PASSES, GROUP_TOKENS], U32, tag="r_codes", bufs=2, align_bytes=64)
+                scales = stage.tile([P, PASSES, GROUP_TOKENS], U8, tag="r_scales", bufs=2, align_bytes=64)
+                r_quantised[group] = (codes, scales)
+            r_codes, r_scales = r_quantised[group]
+            nc.vector.quantize_mx(
+                out=r_codes[:, c, :].bitcast(FP8X4),
+                scales=r_scales[:, c, :],
+                in_=r_grouped[index][:].rearrange("p n t -> p (n t)"),
+            )
+
+        def second_layer(index):
+            if not 0 <= index < N_TILES // 2:
+                return
+            group, pair = divmod(index, GROUP // 2)
+            if pair == 0:
+                x1_sb = stage.tile([P, GROUP, FEATURES], F32, tag="x1_sb", bufs=3)
+                x1_tiles[group] = x1_sb
+            r_codes, r_scales = r_quantised[group]
+            x1_ps = psum.tile([P, 2, FEATURES], F32, tag="x1")
+            for j in range(2):
+                tokens = slice((2 * pair + j) * P, (2 * pair + j + 1) * P)
+                for c in range(PASSES):
+                    nc.tensor.matmul_mx(
+                        out=x1_ps[:, j, :],
+                        lhsT=r_codes[:, c, tokens].bitcast(FP8X4),
+                        lhsT_scale=r_scales[:, c, tokens],
+                        rhs=w2_codes[:, c, :].bitcast(FP8X4),
+                        rhs_scale=w2_scales[:, c, :],
+                        start=(c == 0),
+                        stop=(c == PASSES - 1),
+                    )
+            nc.vector.tensor_tensor(
+                out=x1_tiles[group][:, 2 * pair : 2 * pair + 2, :],
+                in0=x1_ps[:],
+                in1=b2_all.unsqueeze(1).to_broadcast([P, 2, FEATURES]),
+                op=ALU.add,
+            )
+            if pair == GROUP // 2 - 1:
+                rows = slice(group * GROUP_TOKENS, (group + 1) * GROUP_TOKENS)
+                nc.sync.dma_start(
+                    out=out_rows[rows, 0:FEATURES].rearrange("(g p) f -> p g f", p=P),
+                    in_=x1_tiles[group][:],
+                )
+
+        def pool_pair(index):
+            if not 0 <= index < N_TILES // 2:
+                return
+            group, pair = divmod(index, GROUP // 2)
+            if pair == 0:
+                maxima = stage.tile([P, FEATURES // P, GROUP_LINES], F32, tag="line_max", bufs=2)
+                line_max[group] = maxima
+            x1T_ps = psum.tile([P, FEATURES // P, 2 * P], F32, tag="pooled")
+            for s in range(FEATURES // P):
+                for j in range(2):
+                    nc.tensor.transpose(
+                        out=x1T_ps[:, s, j * P : (j + 1) * P],
+                        in_=x1_tiles[group][:, 2 * pair + j, s * P : (s + 1) * P],
+                        identity=ident[:],
+                    )
+            nc.vector.tensor_reduce(
+                out=line_max[group][:, :, pair * PAIR_LINES : (pair + 1) * PAIR_LINES],
+                in_=x1T_ps[:].rearrange("f s (b l) -> f s b l", l=NODES),
+                axis=AXIS.X,
+                op=ALU.max,
+            )
+            if pair == GROUP // 2 - 1:
+                copies = stage.tile([P, FEATURES // P, GROUP_LINES, COPIES], F32, tag="repeated", bufs=2)
+                nc.scalar.copy(
+                    out=copies[:],
+                    in_=line_max[group][:].unsqueeze(3).to_broadcast([P, FEATURES // P, GROUP_LINES, COPIES]),
+                )
+                repeated[group] = copies
+
+        def store_pooled(group):
+            if not 0 <= group < N_GROUPS:
+                return
+            x2_ps = psum.tile([P, FEATURES], F32, tag="pooled")
+            for s in range(FEATURES // P):
+                nc.tensor.transpose(
+                    out=x2_ps[:, s * P : (s + 1) * P],
+                    in_=repeated[group][:, s, :, :].rearrange("f b i -> f (b i)"),
+                    identity=ident[:],
+                )
+            x2_sb = stage.tile([P, FEATURES], F32, tag="x2_sb", bufs=2)
+            nc.scalar.copy(out=x2_sb[:], in_=x2_ps[:])
+            rows = slice(group * GROUP_TOKENS, (group + 1) * GROUP_TOKENS)
+            nodes_each = NODES // COPIES
+            nc.sync.dma_start(
+                out=out_rows[rows, FEATURES : 2 * FEATURES].rearrange("(p m) f -> p m f", m=nodes_each),
+                in_=x2_sb[:].unsqueeze(1).to_broadcast([P, nodes_each, FEATURES]),
+            )
+
+        transpose_x(0)
+
+        bias_all = consts.tile([P, HIDDEN + FEATURES], BF16)
+        for first in range(0, HIDDEN + FEATURES, BANK):
+            width = min(BANK, HIDDEN + FEATURES - first)
+            bias_ps = psum.tile([P, BANK], F32, tag="h", bufs=2)
+            nc.tensor.matmul(
+                out=bias_ps[:, 0:width],
+                lhsT=ones[:],
+                rhs=bias_rows[:, first : first + width],
+                start=True,
+                stop=True,
+            )
+            if first < HIDDEN:
+                nc.scalar.copy(
+                    out=bias_all[:, first : first + width].rearrange("r (t p) -> r t p", t=PACK),
+                    in_=bias_ps[:].rearrange("r (p t) -> r t p", t=PACK),
+                )
+            else:
+                nc.scalar.copy(out=bias_all[:, first : first + width], in_=bias_ps[:, 0:width])
+        b1_all = bias_all[:, 0:HIDDEN]
+        b2_all = bias_all[:, HIDDEN:]
+
+        w1_codes = consts.tile([P, PASSES, HIDDEN], U32, align_bytes=64)
+        w1_scales = consts.tile([P, PASSES, HIDDEN], U8, align_bytes=64)
+
+        def quantise_w1_half(half):
+            cols = slice(half * BANK, (half + 1) * BANK)
+            grouped_passes = []
+            for c in range(PASSES):
+                w1_grouped = stage.tile([P, BANK, PACK], BF16, tag="w1_grouped", bufs=2, align_bytes=64)
+                last = half == HALVES - 1 and c == PASSES - 1
+                copy = nc.scalar.copy if last else nc.vector.tensor_copy
+                regroup(copy, w1_grouped[:], w1_planes[:, PACK * c : PACK * (c + 1), cols])
+                grouped_passes.append(w1_grouped)
+            for c in range(PASSES):
+                nc.vector.quantize_mx(
+                    out=w1_codes[:, c, cols].bitcast(FP8X4),
+                    scales=w1_scales[:, c, cols],
+                    in_=grouped_passes[c][:].rearrange("p n t -> p (n t)"),
+                )
+
+        quantise_w1_half(0)
+        quantise_x(0)
+        affine_f32 = consts.tile([P, PACK, P], F32)
+        nc.vector.tensor_copy(out=affine_f32[:], in_=affine_rows[:].rearrange("r (p t) -> r t p", t=PACK))
+        affine_ps = psum.tile([P, PACK, P], F32, tag="pooled")
+        for t in range(PACK):
+            nc.tensor.transpose(out=affine_ps[:, t, :], in_=affine_f32[:, t, :], identity=ident[:])
+        quantise_w1_half(1)
+        affine_cols = consts.tile([P, PACK, 2 * PASSES], F32)
+        nc.vector.tensor_copy(out=affine_cols[:], in_=affine_ps[:, :, 0 : 2 * PASSES])
+
+        w2_grouped = consts.tile([P, PASSES, FEATURES, PACK], BF16, align_bytes=64)
+        for c in range(PASSES):
+            regroup(nc.scalar.copy, w2_grouped[:, c, :, :], w2_planes[:, PACK * c : PACK * (c + 1), :])
+        w2_codes = consts.tile([P, PASSES, FEATURES], U32, align_bytes=64)
+        w2_scales = consts.tile([P, PASSES, FEATURES], U8, align_bytes=64)
+
+        for step in range(N_STEPS):
+            load_x(step + X_AHEAD)
+            normalise(step - 2)
+            regroup_r(due(step, QUANT_LAG, 2))
+            transpose_x(step + 1)
+            relu_slice(2 * (step - RELU_LAG))
+            relu_slice(2 * (step - RELU_LAG) + 1)
+            pool_pair(due(step, POOL_LAG, 2))
+            store_pooled(due(step, STORE_LAG, GROUP))
+            deviation(step - 1)
+            quantise_x(step + 1)
+            first_layer(step)
+            second_layer(due(step, LAYER2_LAG, 2))
+            quantise_r(due(step, QUANT_LAG, 2))
+            if step == 0:
+                nc.vector.quantize_mx(
+                    out=w2_codes[:].rearrange("p c n -> p (c n)").bitcast(FP8X4),
+                    scales=w2_scales[:].rearrange("p c n -> p (c n)"),
+                    in_=w2_grouped[:].rearrange("p c n t -> p (c n t)"),
+                )

@@ -11,6 +11,7 @@ FP8X4 = mybir.dt.float8_e4m3fn_x4
 ALU = mybir.AluOpType
 ACT = mybir.ActivationFunctionType
 AXIS = mybir.AxisListType
+ENGINE = mybir.EngineType
 
 P = 128
 PACK = 4
@@ -23,34 +24,56 @@ HIDDEN = 1024
 FEATURES = 256
 PASSES = HIDDEN // K_PASS
 SLICES = HIDDEN // P
-GROUP = 4
-GROUP_TOKENS = GROUP * P
-N_GROUPS = TOKENS // GROUP_TOKENS
-GROUP_LINES = GROUP_TOKENS // NODES
-COPIES = P // GROUP_LINES
 EPS = 1e-5
 
 FLOPS = 2 * TOKENS * HIDDEN * (HIDDEN + FEATURES)
 
-
 N_TILES = TOKENS // P
 HALVES = HIDDEN // BANK
-PAIR_LINES = 2 * P // NODES
+GROUPS = [4] * 8
+MAX_GROUP = max(GROUPS)
 
-X_AHEAD = 8
-RELU_LAG = 6
-QUANT_LAG = 8
-LAYER2_LAG = 11
-POOL_LAG = LAYER2_LAG + 2
-STORE_LAG = POOL_LAG + 3
-N_STEPS = N_TILES - GROUP + STORE_LAG + 1
-SCALAR_SHARE = 4
+X_LOADS_AHEAD = 8
+X_AHEAD = 2
 
 
-def due(step, lag, period):
-    if step < lag or (step - lag) % period != 0:
-        return -1
-    return (step - lag) // period
+def plan():
+    table = {}
+
+    def add(step, stage, piece):
+        table.setdefault((step, stage), []).append(piece)
+
+    step, units, first, last_step = 0, 0, 0, 0
+    for g, size in enumerate(GROUPS):
+        last = first + size - 1
+        first += size
+        cut = 3 if last >= N_TILES - 4 else 0
+        earliest = last + max(3 - cut, 1)
+        if earliest > step:
+            step, units = earliest, 0
+        done = []
+        for s in range(SLICES):
+            if units + size > 8:
+                step, units = step + 1, 0
+            add(step, "relu", (g, s))
+            units += size
+            done.append(step)
+        regroup_lag = max(1 - cut, 1)
+        for half in range(PASSES):
+            at = done[PACK * (half + 1) - 1] + regroup_lag
+            add(at, "regroup", (g, half))
+            add(at + 2, "quantise", (g, half))
+        at = done[-1] + regroup_lag + 2 + 1
+        spacing = 1 if cut else 1
+        pairs = (size + 1) // 2
+        for pair in range(pairs):
+            add(at + spacing * pair, "layer2", (g, pair))
+            add(at + spacing * pair + 3, "pool", (g, pair))
+        at += spacing * (pairs - 1) + 3 + 1
+        add(at, "repeat", g)
+        add(at + 2, "store", g)
+        last_step = max(last_step, at + 2)
+    return table, last_step
 
 
 def regroup(copy, grouped, planes):
@@ -64,79 +87,87 @@ def tile_sub_graph_pa_t_kernel(tc, x_nodes, w1, b1, gamma, beta, w2, b2, out):
     nc = tc.nc
     x_rows = x_nodes.flatten_outer_dims()
     out_rows = out.flatten_outer_dims()
+    table, last_step = plan()
+    group_first = [sum(GROUPS[:g]) for g in range(len(GROUPS))]
 
     with ExitStack() as ctx:
         consts = ctx.enter_context(tc.tile_pool(name="consts", bufs=1))
         stage = ctx.enter_context(tc.tile_pool(name="stage", bufs=2))
         psum = ctx.enter_context(tc.psum_pool(name="psum", bufs=1))
+        ctx.enter_context(tc.manual_schedule())
 
         x_tiles, x_words, x_quantised = {}, {}, {}
-        normed, row_sums, minus_mean, inv_std = {}, {}, {}, {}
+        normed, row_sums, minus_mean, squared, inv_std, gates = {}, {}, {}, {}, {}, {}
         r_planes, r_grouped, r_quantised = {}, {}, {}
         x1_tiles, line_max, repeated = {}, {}, {}
 
         def load_x(i):
             if i >= N_TILES:
                 return
-            x_sb = stage.tile([P, HIDDEN], BF16, tag="x_sb", bufs=X_AHEAD + 2)
+            x_sb = stage.tile([P, HIDDEN], BF16, tag="x_sb", bufs=X_LOADS_AHEAD + 2)
             nc.sync.dma_start(out=x_sb[:], in_=x_rows[i * P : (i + 1) * P, :])
             x_tiles[i] = x_sb
 
-        w1_planes = consts.tile([P, PASSES * PACK, HIDDEN], BF16)
         w1_passes = w1.rearrange("(c p t) n -> c p t n", c=PASSES, p=P, t=PACK)
+        w1_planes = {}
 
-        def load_w1_half(half):
+        def load_w1(c, half):
             cols = slice(half * BANK, (half + 1) * BANK)
-            for c in range(PASSES):
-                nc.sync.dma_start(
-                    out=w1_planes[:, PACK * c : PACK * (c + 1), cols], in_=w1_passes[c][:, :, cols]
-                )
+            planes = consts.tile([P, PACK, BANK], BF16, name="w1_planes_%d%d" % (c, half))
+            nc.sync.dma_start(out=planes[:], in_=w1_passes[c][:, :, cols])
+            w1_planes[c, half] = planes
 
-        affine_rows = consts.tile([P, K_PASS], BF16)
-        nc.vector.memset(affine_rows[:], 0.0)
-        eps = consts.tile([P, 1], F32)
-        nc.vector.memset(eps[:], EPS)
-        ident = consts.tile([P, P], F32)
-        make_identity(nc, ident[:])
+        load_w1(0, 0)
+        load_x(0)
+        load_w1(1, 0)
 
-        nc.scalar.dma_start(out=affine_rows[0:PASSES, :], in_=gamma.rearrange("(c n) -> c n", c=PASSES))
-        nc.scalar.dma_start(
-            out=affine_rows[PASSES : 2 * PASSES, :], in_=beta.rearrange("(c n) -> c n", c=PASSES)
-        )
         bias_rows = consts.tile([P, HIDDEN + FEATURES], BF16)
-        nc.vector.memset(bias_rows[:], 0.0)
+        nc.vector.memset(bias_rows[:].bitcast(U32), 0)
+        affine_rows = consts.tile([P, K_PASS], BF16)
+        nc.vector.memset(affine_rows[:].bitcast(U32), 0)
         ones = consts.tile([P, P], BF16)
         nc.vector.memset(ones[:], 1.0)
+        eps = consts.tile([P, 1], F32)
+        nc.vector.memset(eps[:], EPS)
+        warm = consts.tile([P, 1], F32)
+        nc.scalar.activation(out=warm[:], in_=eps[:], func=ACT.Abs_reciprocal_sqrt)
+        ident = consts.tile([P, P], F32)
+        make_identity(nc, ident[:])
         nc.scalar.dma_start(out=bias_rows[0:1, 0:HIDDEN], in_=b1.rearrange("(o n) -> o n", o=1))
         nc.scalar.dma_start(out=bias_rows[0:1, HIDDEN:], in_=b2.rearrange("(o n) -> o n", o=1))
+        nc.scalar.dma_start(out=affine_rows[0:PASSES, :], in_=gamma.rearrange("(c n) -> c n", c=PASSES))
+        nc.scalar.dma_start(out=affine_rows[PASSES : 2 * PASSES, :], in_=beta.rearrange("(c n) -> c n", c=PASSES))
 
-        load_x(0)
-        load_w1_half(0)
+        load_w1(0, 1)
+        load_w1(1, 1)
         load_x(1)
-        load_w1_half(1)
+        load_x(2)
         w2_planes = consts.tile([P, PASSES * PACK, FEATURES], BF16)
         for c in range(PASSES):
             nc.sync.dma_start(
                 out=w2_planes[:, PACK * c : PACK * (c + 1), :],
                 in_=w2[c * K_PASS : (c + 1) * K_PASS, :].rearrange("(p t) n -> p t n", t=PACK),
             )
-        for i in range(2, X_AHEAD):
+        for i in range(3, X_LOADS_AHEAD):
             load_x(i)
 
         def transpose_x(i):
             if i >= N_TILES:
                 return
             words = x_tiles[i][:].bitcast(F32)
-            xT_ps = psum.tile([P, PASSES, 2, P], F32, tag="xT", bufs=2)
+            xT_ps = psum.tile([P, PASSES, 2, P], F32, tag="xT", bufs=1)
             for c in range(PASSES):
                 for u in range(2):
                     nc.tensor.transpose(
-                        out=xT_ps[:, c, u, :],
-                        in_=words[:, 2 * P * c + u : 2 * P * (c + 1) : 2],
-                        identity=ident[:],
+                        out=xT_ps[:, c, u, :], in_=words[:, 2 * P * c + u : 2 * P * (c + 1) : 2], identity=ident[:]
                     )
+            x_words[i] = xT_ps
+
+        def copy_x(i):
+            if i >= N_TILES:
+                return
             x_grouped = stage.tile([P, PASSES, P, 2], F32, tag="x_grouped", bufs=3, align_bytes=64)
-            nc.scalar.copy(out=x_grouped[:], in_=xT_ps[:].rearrange("q c u r -> q c r u"))
+            nc.scalar.copy(out=x_grouped[:], in_=x_words[i][:].rearrange("q c u r -> q c r u"))
             x_words[i] = x_grouped
 
         def quantise_x(i):
@@ -151,12 +182,12 @@ def tile_sub_graph_pa_t_kernel(tc, x_nodes, w1, b1, gamma, beta, w2, b2, out):
             )
             x_quantised[i] = (x_codes, x_scales)
 
-        def first_layer(i):
+        h_banks = {}
+
+        def layer1(i):
             if i >= N_TILES:
                 return
             x_codes, x_scales = x_quantised[i]
-            biased = stage.tile([P, HIDDEN], F32, tag="normed", bufs=12)
-            sums = stage.tile([P, HALVES], F32, tag="sums", bufs=4)
             for half in range(HALVES):
                 cols = slice(half * BANK, (half + 1) * BANK)
                 h_ps = psum.tile([P, BANK], F32, tag="h", bufs=2)
@@ -170,9 +201,18 @@ def tile_sub_graph_pa_t_kernel(tc, x_nodes, w1, b1, gamma, beta, w2, b2, out):
                         start=(c == 0),
                         stop=(c == PASSES - 1),
                     )
+                h_banks[i, half] = h_ps
+
+        def evacuate_h(i):
+            if i >= N_TILES:
+                return
+            biased = stage.tile([P, HIDDEN], F32, tag="normed", bufs=14)
+            sums = stage.tile([P, HALVES], F32, tag="sums", bufs=8)
+            for half in range(HALVES):
+                cols = slice(half * BANK, (half + 1) * BANK)
                 nc.vector.scalar_tensor_tensor(
                     out=biased[:, cols].rearrange("r (t p) -> r t p", t=PACK),
-                    in0=h_ps[:].rearrange("r (p t) -> r t p", t=PACK),
+                    in0=h_banks[i, half][:].rearrange("r (p t) -> r t p", t=PACK),
                     scalar=1.0,
                     in1=b1_all[:, cols].rearrange("r (t p) -> r t p", t=PACK),
                     op0=ALU.mult,
@@ -182,21 +222,25 @@ def tile_sub_graph_pa_t_kernel(tc, x_nodes, w1, b1, gamma, beta, w2, b2, out):
             normed[i] = biased
             row_sums[i] = sums
 
-        def deviation(i):
+        def mean(i):
             if not 0 <= i < N_TILES:
                 return
-            scaled_sums = stage.tile([P, HALVES], F32, tag="scaled_sums", bufs=2)
-            negated = stage.tile([P, 1], F32, tag="minus_mean", bufs=6)
-            nc.scalar.activation(
-                out=scaled_sums[:],
-                in_=row_sums[i][:],
-                func=ACT.Identity,
-                scale=-1.0 / HIDDEN,
-                accum_out=negated[:, 0:1],
+            negated = stage.tile([P, 1], F32, tag="minus_mean", bufs=8)
+            nc.vector.tensor_scalar(
+                out=negated[:],
+                in0=row_sums[i][:, 0:1],
+                scalar1=row_sums[i][:, 1:2],
+                scalar2=-1.0 / HIDDEN,
+                op0=ALU.add,
+                op1=ALU.mult,
             )
             minus_mean[i] = negated
+
+        def square(i):
+            if not 0 <= i < N_TILES:
+                return
             squares = stage.tile([P, HIDDEN], BF16, tag="squares", bufs=2)
-            sum_sq = stage.tile([P, 1], F32, tag="sum_sq", bufs=3)
+            sum_sq = stage.tile([P, 1], F32, tag="sum_sq", bufs=4)
             nc.scalar.activation(
                 out=squares[:],
                 in_=normed[i][:],
@@ -205,10 +249,15 @@ def tile_sub_graph_pa_t_kernel(tc, x_nodes, w1, b1, gamma, beta, w2, b2, out):
                 scale=1.0,
                 accum_out=sum_sq[:, 0:1],
             )
-            inverse = stage.tile([P, 1], F32, tag="inv_std", bufs=4)
+            squared[i] = sum_sq
+
+        def deviation(i):
+            if not 0 <= i < N_TILES:
+                return
+            inverse = stage.tile([P, 1], F32, tag="inv_std", bufs=6)
             nc.scalar.activation(
                 out=inverse[:],
-                in_=sum_sq[:],
+                in_=squared[i][:],
                 func=ACT.Abs_reciprocal_sqrt,
                 bias=eps[:, 0:1],
                 scale=1.0 / HIDDEN,
@@ -218,81 +267,74 @@ def tile_sub_graph_pa_t_kernel(tc, x_nodes, w1, b1, gamma, beta, w2, b2, out):
         def normalise(i):
             if not 0 <= i < N_TILES:
                 return
-            if i % SCALAR_SHARE == 0:
-                shift = stage.tile([P, 1], F32, tag="shift", bufs=2)
-                nc.scalar.mul(out=shift[:], in_=minus_mean[i][:], mul=inv_std[i][:, 0:1])
-                nc.scalar.activation(
-                    out=normed[i][:],
-                    in_=normed[i][:],
-                    func=ACT.Identity,
-                    bias=shift[:, 0:1],
-                    scale=inv_std[i][:, 0:1],
-                )
-                return
-            nc.vector.tensor_scalar(
+            gate = stage.tile([P, 1], F32, tag="gate", bufs=4)
+            nc.vector.tensor_copy(out=gate[:], in_=inv_std[i][:])
+            nc.gpsimd.tensor_scalar(
                 out=normed[i][:],
                 in0=normed[i][:],
                 scalar1=minus_mean[i][:, 0:1],
-                scalar2=inv_std[i][:, 0:1],
+                scalar2=gate[:, 0:1],
                 op0=ALU.add,
                 op1=ALU.mult,
             )
 
-        def relu_slice(index):
-            if not 0 <= index < N_GROUPS * SLICES:
-                return
-            group, s = divmod(index, SLICES)
-            if s == 0:
-                planes = stage.tile([P, SLICES, GROUP_TOKENS], BF16, tag="r_planes", bufs=2)
-                r_planes[group] = planes
-            normedT_ps = psum.tile([P, GROUP_TOKENS], F32, tag="normedT", bufs=2)
-            for g in range(GROUP):
+        normedT = {}
+
+        def transpose_h(piece):
+            g, s = piece
+            size = GROUPS[g]
+            normedT_ps = psum.tile([P, MAX_GROUP * P], F32, tag="normedT", bufs=3)
+            for k in range(size):
                 nc.tensor.transpose(
-                    out=normedT_ps[:, g * P : (g + 1) * P],
-                    in_=normed[group * GROUP + g][:, s * P : (s + 1) * P],
+                    out=normedT_ps[:, k * P : (k + 1) * P],
+                    in_=normed[group_first[g] + k][:, s * P : (s + 1) * P],
                     identity=ident[:],
                 )
+            normedT[piece] = normedT_ps
+
+        def relu(piece):
+            g, s = piece
+            if s == 0:
+                planes = stage.tile([P, SLICES, MAX_GROUP * P], BF16, tag="r_planes", bufs=2)
+                r_planes[g] = planes
+            width = GROUPS[g] * P
+            c, t = divmod(s, PACK)
             nc.scalar.activation(
-                out=r_planes[group][:, s, :],
-                in_=normedT_ps[:],
+                out=r_planes[g][:, s, 0:width],
+                in_=normedT[piece][:, 0:width],
                 func=ACT.Relu,
-                bias=affine_cols[:, s % PACK, PASSES + s // PACK : PASSES + s // PACK + 1],
-                scale=affine_cols[:, s % PACK, s // PACK : s // PACK + 1],
+                bias=affine_cols[:, t, PASSES + c : PASSES + c + 1],
+                scale=affine_cols[:, t, c : c + 1],
             )
 
-        def regroup_r(index):
-            if not 0 <= index < N_GROUPS * PASSES:
-                return
-            group, c = divmod(index, PASSES)
-            grouped = stage.tile([P, GROUP_TOKENS, PACK], BF16, tag="r_grouped", bufs=2, align_bytes=64)
-            regroup(nc.vector.tensor_copy, grouped[:], r_planes[group][:, PACK * c : PACK * (c + 1), :])
-            r_grouped[index] = grouped
+        def regroup_r(piece):
+            g, c = piece
+            width = GROUPS[g] * P
+            grouped = stage.tile([P, MAX_GROUP * P, PACK], BF16, tag="r_grouped", bufs=2, align_bytes=64)
+            regroup(nc.vector.tensor_copy, grouped[:, 0:width, :], r_planes[g][:, PACK * c : PACK * (c + 1), 0:width])
+            r_grouped[piece] = grouped
 
-        def quantise_r(index):
-            if not 0 <= index < N_GROUPS * PASSES:
-                return
-            group, c = divmod(index, PASSES)
+        def quantise_r(piece):
+            g, c = piece
+            width = GROUPS[g] * P
             if c == 0:
-                codes = stage.tile([P, PASSES, GROUP_TOKENS], U32, tag="r_codes", bufs=2, align_bytes=64)
-                scales = stage.tile([P, PASSES, GROUP_TOKENS], U8, tag="r_scales", bufs=2, align_bytes=64)
-                r_quantised[group] = (codes, scales)
-            r_codes, r_scales = r_quantised[group]
+                codes = stage.tile([P, PASSES, MAX_GROUP * P], U32, tag="r_codes", bufs=2, align_bytes=64)
+                scales = stage.tile([P, PASSES, MAX_GROUP * P], U8, tag="r_scales", bufs=2, align_bytes=64)
+                r_quantised[g] = (codes, scales)
+            r_codes, r_scales = r_quantised[g]
             nc.vector.quantize_mx(
-                out=r_codes[:, c, :].bitcast(FP8X4),
-                scales=r_scales[:, c, :],
-                in_=r_grouped[index][:].rearrange("p n t -> p (n t)"),
+                out=r_codes[:, c, 0:width].bitcast(FP8X4),
+                scales=r_scales[:, c, 0:width],
+                in_=r_grouped[piece][:, 0:width, :].rearrange("p n t -> p (n t)"),
             )
 
-        def second_layer(index):
-            if not 0 <= index < N_TILES // 2:
-                return
-            group, pair = divmod(index, GROUP // 2)
-            if pair == 0:
-                x1_sb = stage.tile([P, GROUP, FEATURES], F32, tag="x1_sb", bufs=3)
-                x1_tiles[group] = x1_sb
-            r_codes, r_scales = r_quantised[group]
+        x1_banks = {}
+
+        def layer2(piece):
+            g, pair = piece
+            r_codes, r_scales = r_quantised[g]
             x1_ps = psum.tile([P, 2, FEATURES], F32, tag="x1")
-            for j in range(2):
+            for j in range(min(2, GROUPS[g] - 2 * pair)):
                 tokens = slice((2 * pair + j) * P, (2 * pair + j + 1) * P)
                 for c in range(PASSES):
                     nc.tensor.matmul_mx(
@@ -304,71 +346,86 @@ def tile_sub_graph_pa_t_kernel(tc, x_nodes, w1, b1, gamma, beta, w2, b2, out):
                         start=(c == 0),
                         stop=(c == PASSES - 1),
                     )
+            x1_banks[piece] = x1_ps
+
+        def evacuate_x1(piece):
+            g, pair = piece
+            size = GROUPS[g]
+            if pair == 0:
+                x1_sb = stage.tile([P, MAX_GROUP, FEATURES], F32, tag="x1_sb", bufs=3)
+                x1_tiles[g] = x1_sb
+            count = min(2, size - 2 * pair)
             nc.vector.tensor_tensor(
-                out=x1_tiles[group][:, 2 * pair : 2 * pair + 2, :],
-                in0=x1_ps[:],
-                in1=b2_all.unsqueeze(1).to_broadcast([P, 2, FEATURES]),
+                out=x1_tiles[g][:, 2 * pair : 2 * pair + count, :],
+                in0=x1_banks[piece][:, 0:count, :],
+                in1=b2_all.unsqueeze(1).to_broadcast([P, count, FEATURES]),
                 op=ALU.add,
             )
-            if pair == GROUP // 2 - 1:
-                rows = slice(group * GROUP_TOKENS, (group + 1) * GROUP_TOKENS)
+            if 2 * pair + count == size:
+                rows = slice(group_first[g] * P, (group_first[g] + size) * P)
                 nc.sync.dma_start(
                     out=out_rows[rows, 0:FEATURES].rearrange("(g p) f -> p g f", p=P),
-                    in_=x1_tiles[group][:],
+                    in_=x1_tiles[g][:, 0:size, :],
                 )
 
-        def pool_pair(index):
-            if not 0 <= index < N_TILES // 2:
-                return
-            group, pair = divmod(index, GROUP // 2)
-            if pair == 0:
-                maxima = stage.tile([P, FEATURES // P, GROUP_LINES], F32, tag="line_max", bufs=2)
-                line_max[group] = maxima
+        pooled_banks = {}
+
+        def transpose_x1(piece):
+            g, pair = piece
             x1T_ps = psum.tile([P, FEATURES // P, 2 * P], F32, tag="pooled")
             for s in range(FEATURES // P):
-                for j in range(2):
+                for j in range(min(2, GROUPS[g] - 2 * pair)):
                     nc.tensor.transpose(
                         out=x1T_ps[:, s, j * P : (j + 1) * P],
-                        in_=x1_tiles[group][:, 2 * pair + j, s * P : (s + 1) * P],
+                        in_=x1_tiles[g][:, 2 * pair + j, s * P : (s + 1) * P],
                         identity=ident[:],
                     )
+            pooled_banks[piece] = x1T_ps
+
+        def pool(piece):
+            g, pair = piece
+            size = GROUPS[g]
+            lines = size * P // NODES
+            if pair == 0:
+                maxima = stage.tile([P, FEATURES // P, MAX_GROUP * P // NODES], F32, tag="line_max", bufs=2)
+                line_max[g] = maxima
+            count = min(2, size - 2 * pair)
+            first = 2 * pair * P // NODES
             nc.vector.tensor_reduce(
-                out=line_max[group][:, :, pair * PAIR_LINES : (pair + 1) * PAIR_LINES],
-                in_=x1T_ps[:].rearrange("f s (b l) -> f s b l", l=NODES),
+                out=line_max[g][:, :, first : first + count * P // NODES],
+                in_=pooled_banks[piece][:, :, 0 : count * P].rearrange("f s (b l) -> f s b l", l=NODES),
                 axis=AXIS.X,
                 op=ALU.max,
             )
-            if pair == GROUP // 2 - 1:
-                copies = stage.tile([P, FEATURES // P, GROUP_LINES, COPIES], F32, tag="repeated", bufs=2)
-                nc.scalar.copy(
-                    out=copies[:],
-                    in_=line_max[group][:].unsqueeze(3).to_broadcast([P, FEATURES // P, GROUP_LINES, COPIES]),
-                )
-                repeated[group] = copies
 
-        def store_pooled(group):
-            if not 0 <= group < N_GROUPS:
-                return
+        def repeat(g):
+            lines = GROUPS[g] * P // NODES
+            copies = P // lines
+            rep = stage.tile([P, FEATURES // P, P], F32, tag="repeated", bufs=2)
+            nc.scalar.copy(
+                out=rep[:].rearrange("f s (b i) -> f s b i", i=copies),
+                in_=line_max[g][:, :, 0:lines].unsqueeze(3).to_broadcast([P, FEATURES // P, lines, copies]),
+            )
+            repeated[g] = rep
+
+        def store_pooled(g):
+            size = GROUPS[g]
             x2_ps = psum.tile([P, FEATURES], F32, tag="pooled")
             for s in range(FEATURES // P):
                 nc.tensor.transpose(
-                    out=x2_ps[:, s * P : (s + 1) * P],
-                    in_=repeated[group][:, s, :, :].rearrange("f b i -> f (b i)"),
-                    identity=ident[:],
+                    out=x2_ps[:, s * P : (s + 1) * P], in_=repeated[g][:, s, :], identity=ident[:]
                 )
             x2_sb = stage.tile([P, FEATURES], F32, tag="x2_sb", bufs=2)
             nc.scalar.copy(out=x2_sb[:], in_=x2_ps[:])
-            rows = slice(group * GROUP_TOKENS, (group + 1) * GROUP_TOKENS)
-            nodes_each = NODES // COPIES
+            rows = slice(group_first[g] * P, (group_first[g] + size) * P)
             nc.sync.dma_start(
-                out=out_rows[rows, FEATURES : 2 * FEATURES].rearrange("(p m) f -> p m f", m=nodes_each),
-                in_=x2_sb[:].unsqueeze(1).to_broadcast([P, nodes_each, FEATURES]),
+                out=out_rows[rows, FEATURES : 2 * FEATURES].rearrange("(p m) f -> p m f", m=size),
+                in_=x2_sb[:].unsqueeze(1).to_broadcast([P, size, FEATURES]),
             )
 
-        transpose_x(0)
-
         bias_all = consts.tile([P, HIDDEN + FEATURES], BF16)
-        for first in range(0, HIDDEN + FEATURES, BANK):
+
+        def spread_bias(first):
             width = min(BANK, HIDDEN + FEATURES - first)
             bias_ps = psum.tile([P, BANK], F32, tag="h", bufs=2)
             nc.tensor.matmul(
@@ -385,60 +442,108 @@ def tile_sub_graph_pa_t_kernel(tc, x_nodes, w1, b1, gamma, beta, w2, b2, out):
                 )
             else:
                 nc.scalar.copy(out=bias_all[:, first : first + width], in_=bias_ps[:, 0:width])
+
         b1_all = bias_all[:, 0:HIDDEN]
         b2_all = bias_all[:, HIDDEN:]
 
         w1_codes = consts.tile([P, PASSES, HIDDEN], U32, align_bytes=64)
         w1_scales = consts.tile([P, PASSES, HIDDEN], U8, align_bytes=64)
+        w1_grouped = {}
 
-        def quantise_w1_half(half):
+        def regroup_w1(c, half):
+            grouped = stage.tile([P, BANK, PACK], BF16, tag="w1_grouped", bufs=2, align_bytes=64)
+            split = 320
+            planes = w1_planes[c, half]
+            regroup(nc.vector.tensor_copy, grouped[:, 0:split, :], planes[:, :, 0:split])
+            regroup(nc.scalar.copy, grouped[:, split:BANK, :], planes[:, :, split:BANK])
+            w1_grouped[c, half] = grouped
+
+        def quantise_w1(c, half):
             cols = slice(half * BANK, (half + 1) * BANK)
-            grouped_passes = []
-            for c in range(PASSES):
-                w1_grouped = stage.tile([P, BANK, PACK], BF16, tag="w1_grouped", bufs=2, align_bytes=64)
-                last = half == HALVES - 1 and c == PASSES - 1
-                copy = nc.scalar.copy if last else nc.vector.tensor_copy
-                regroup(copy, w1_grouped[:], w1_planes[:, PACK * c : PACK * (c + 1), cols])
-                grouped_passes.append(w1_grouped)
-            for c in range(PASSES):
-                nc.vector.quantize_mx(
-                    out=w1_codes[:, c, cols].bitcast(FP8X4),
-                    scales=w1_scales[:, c, cols],
-                    in_=grouped_passes[c][:].rearrange("p n t -> p (n t)"),
-                )
+            nc.vector.quantize_mx(
+                out=w1_codes[:, c, cols].bitcast(FP8X4),
+                scales=w1_scales[:, c, cols],
+                in_=w1_grouped[c, half][:].rearrange("p n t -> p (n t)"),
+            )
 
-        quantise_w1_half(0)
+        transpose_x(0)
+        regroup_w1(0, 0)
+        copy_x(0)
+        spread_bias(0)
+        regroup_w1(1, 0)
+        quantise_w1(0, 0)
         quantise_x(0)
-        affine_f32 = consts.tile([P, PACK, P], F32)
-        nc.vector.tensor_copy(out=affine_f32[:], in_=affine_rows[:].rearrange("r (p t) -> r t p", t=PACK))
-        affine_ps = psum.tile([P, PACK, P], F32, tag="pooled")
-        for t in range(PACK):
-            nc.tensor.transpose(out=affine_ps[:, t, :], in_=affine_f32[:, t, :], identity=ident[:])
-        quantise_w1_half(1)
-        affine_cols = consts.tile([P, PACK, 2 * PASSES], F32)
-        nc.vector.tensor_copy(out=affine_cols[:], in_=affine_ps[:, :, 0 : 2 * PASSES])
+        spread_bias(BANK)
+        quantise_w1(1, 0)
+        regroup_w1(0, 1)
+        regroup_w1(1, 1)
+        quantise_w1(0, 1)
+        quantise_w1(1, 1)
+        for i in range(1, X_AHEAD):
+            transpose_x(i)
+            copy_x(i)
 
+        affine_f32 = consts.tile([P, PACK, P], F32)
+        affine_cols = consts.tile([P, PACK, 2 * PASSES], F32)
         w2_grouped = consts.tile([P, PASSES, FEATURES, PACK], BF16, align_bytes=64)
-        for c in range(PASSES):
-            regroup(nc.scalar.copy, w2_grouped[:, c, :, :], w2_planes[:, PACK * c : PACK * (c + 1), :])
         w2_codes = consts.tile([P, PASSES, FEATURES], U32, align_bytes=64)
         w2_scales = consts.tile([P, PASSES, FEATURES], U8, align_bytes=64)
 
-        for step in range(N_STEPS):
-            load_x(step + X_AHEAD)
-            normalise(step - 2)
-            regroup_r(due(step, QUANT_LAG, 2))
-            transpose_x(step + 1)
-            relu_slice(2 * (step - RELU_LAG))
-            relu_slice(2 * (step - RELU_LAG) + 1)
-            pool_pair(due(step, POOL_LAG, 2))
-            store_pooled(due(step, STORE_LAG, GROUP))
-            deviation(step - 1)
+        def load_affine():
+            nc.vector.tensor_copy(out=affine_f32[:], in_=affine_rows[:].rearrange("r (p t) -> r t p", t=PACK))
+            affine_ps = psum.tile([P, PACK, P], F32, tag="pooled")
+            for t in range(PACK):
+                nc.tensor.transpose(out=affine_ps[:, t, :], in_=affine_f32[:, t, :], identity=ident[:])
+            nc.vector.tensor_copy(out=affine_cols[:], in_=affine_ps[:, :, 0 : 2 * PASSES])
+
+        for step in range(last_step + 1):
+
+            def due(stage_name):
+                return table.get((step, stage_name), [])
+
+            load_x(step + X_LOADS_AHEAD)
+            pieces = due("relu")
             quantise_x(step + 1)
-            first_layer(step)
-            second_layer(due(step, LAYER2_LAG, 2))
-            quantise_r(due(step, QUANT_LAG, 2))
+            for piece in due("quantise"):
+                quantise_r(piece)
+            for piece in due("regroup"):
+                regroup_r(piece)
+            normalise(step - 2)
+            mean(step - 1)
+            transpose_x(step + X_AHEAD)
+            for piece in pieces[0:2]:
+                transpose_h(piece)
+            for piece in due("pool"):
+                transpose_x1(piece)
+            layer1(step)
+            for piece in due("layer2"):
+                layer2(piece)
+            for piece in pieces[0:1]:
+                relu(piece)
+            for g in due("repeat"):
+                repeat(g)
+            copy_x(step + X_AHEAD)
+            square(step - 1)
+            for g in due("store"):
+                store_pooled(g)
+            for piece in pieces[1:2]:
+                relu(piece)
+            for piece in pieces[2:]:
+                transpose_h(piece)
+                relu(piece)
+            deviation(step - 1)
+            for piece in due("pool"):
+                pool(piece)
+            evacuate_h(step)
+            for piece in due("layer2"):
+                evacuate_x1(piece)
             if step == 0:
+                spread_bias(2 * BANK)
+            if step == 1:
+                load_affine()
+                for c in range(PASSES):
+                    regroup(nc.vector.tensor_copy, w2_grouped[:, c, :, :], w2_planes[:, PACK * c : PACK * (c + 1), :])
+            if step == 2:
                 nc.vector.quantize_mx(
                     out=w2_codes[:].rearrange("p c n -> p (c n)").bitcast(FP8X4),
                     scales=w2_scales[:].rearrange("p c n -> p (c n)"),

@@ -11,7 +11,6 @@ FP8X4 = mybir.dt.float8_e4m3fn_x4
 ALU = mybir.AluOpType
 ACT = mybir.ActivationFunctionType
 AXIS = mybir.AxisListType
-ENGINE = mybir.EngineType
 
 P = 128
 PACK = 4
@@ -28,52 +27,28 @@ EPS = 1e-5
 
 FLOPS = 2 * TOKENS * HIDDEN * (HIDDEN + FEATURES)
 
-N_TILES = TOKENS // P
+PAIR = 2
+PAIR_TOKENS = PAIR * P
+N_PAIRS = TOKENS // PAIR_TOKENS
 HALVES = HIDDEN // BANK
-GROUPS = [4] * 8
-MAX_GROUP = max(GROUPS)
+FEATURE_SLICES = FEATURES // P
 
-X_LOADS_AHEAD = 8
-X_AHEAD = 2
+BATCH = 2
+BATCH_LINES = BATCH * PAIR_TOKENS // NODES
+COPIES = P // BATCH_LINES
+BATCH_TOKENS = BATCH * PAIR_TOKENS
 
-
-def plan():
-    table = {}
-
-    def add(step, stage, piece):
-        table.setdefault((step, stage), []).append(piece)
-
-    step, units, first, last_step = 0, 0, 0, 0
-    for g, size in enumerate(GROUPS):
-        last = first + size - 1
-        first += size
-        cut = 3 if last >= N_TILES - 4 else 0
-        earliest = last + max(3 - cut, 1)
-        if earliest > step:
-            step, units = earliest, 0
-        done = []
-        for s in range(SLICES):
-            if units + size > 8:
-                step, units = step + 1, 0
-            add(step, "relu", (g, s))
-            units += size
-            done.append(step)
-        regroup_lag = max(1 - cut, 1)
-        for half in range(PASSES):
-            at = done[PACK * (half + 1) - 1] + regroup_lag
-            add(at, "regroup", (g, half))
-            add(at + 2, "quantise", (g, half))
-        at = done[-1] + regroup_lag + 2 + 1
-        spacing = 1 if cut else 1
-        pairs = (size + 1) // 2
-        for pair in range(pairs):
-            add(at + spacing * pair, "layer2", (g, pair))
-            add(at + spacing * pair + 3, "pool", (g, pair))
-        at += spacing * (pairs - 1) + 3 + 1
-        add(at, "repeat", g)
-        add(at + 2, "store", g)
-        last_step = max(last_step, at + 2)
-    return table, last_step
+NORM = 2
+RELU = 3
+REGROUP = 4
+QUANT = 4
+LAYER2 = 4
+X1_OUT = 4
+POOL = 5
+REPEAT = 6
+STORE = 6
+N_STEPS = N_PAIRS + STORE
+X_LOADS_AHEAD = 4
 
 
 def regroup(copy, grouped, planes):
@@ -87,8 +62,6 @@ def tile_sub_graph_pa_t_kernel(tc, x_nodes, w1, b1, gamma, beta, w2, b2, out):
     nc = tc.nc
     x_rows = x_nodes.flatten_outer_dims()
     out_rows = out.flatten_outer_dims()
-    table, last_step = plan()
-    group_first = [sum(GROUPS[:g]) for g in range(len(GROUPS))]
 
     with ExitStack() as ctx:
         consts = ctx.enter_context(tc.tile_pool(name="consts", bufs=1))
@@ -96,17 +69,22 @@ def tile_sub_graph_pa_t_kernel(tc, x_nodes, w1, b1, gamma, beta, w2, b2, out):
         psum = ctx.enter_context(tc.psum_pool(name="psum", bufs=1))
         ctx.enter_context(tc.manual_schedule())
 
-        x_tiles, x_words, x_quantised = {}, {}, {}
-        normed, row_sums, minus_mean, squared, inv_std, gates = {}, {}, {}, {}, {}, {}
-        r_planes, r_grouped, r_quantised = {}, {}, {}
-        x1_tiles, line_max, repeated = {}, {}, {}
+        x_tiles, x_banks, x_words, x_quantised = {}, {}, {}, {}
+        normed, row_sums, minus_mean, squared, inv_std = {}, {}, {}, {}, {}
+        h_banks, r_planes, r_grouped, r_quantised = {}, {}, {}, {}
+        x1_banks, x1_tiles, pooled_banks, line_max, repeated = {}, {}, {}, {}, {}
 
-        def load_x(i):
-            if i >= N_TILES:
+        def is_pair(p):
+            return 0 <= p < N_PAIRS
+
+        def load_x(p, k):
+            if not is_pair(p):
                 return
-            x_sb = stage.tile([P, HIDDEN], BF16, tag="x_sb", bufs=X_LOADS_AHEAD + 2)
-            nc.sync.dma_start(out=x_sb[:], in_=x_rows[i * P : (i + 1) * P, :])
-            x_tiles[i] = x_sb
+            if k == 0:
+                x_pair = stage.tile([P, PAIR, HIDDEN], BF16, tag="x_sb", bufs=X_LOADS_AHEAD + 1)
+                x_tiles[p] = x_pair
+            first = p * PAIR_TOKENS + k * P
+            nc.sync.dma_start(out=x_tiles[p][:, k, :], in_=x_rows[first : first + P, :])
 
         w1_passes = w1.rearrange("(c p t) n -> c p t n", c=PASSES, p=P, t=PACK)
         w1_planes = {}
@@ -118,8 +96,7 @@ def tile_sub_graph_pa_t_kernel(tc, x_nodes, w1, b1, gamma, beta, w2, b2, out):
             w1_planes[c, half] = planes
 
         load_w1(0, 0)
-        load_x(0)
-        load_w1(1, 0)
+        load_x(0, 0)
 
         bias_rows = consts.tile([P, HIDDEN + FEATURES], BF16)
         nc.vector.memset(bias_rows[:].bitcast(U32), 0)
@@ -133,294 +110,294 @@ def tile_sub_graph_pa_t_kernel(tc, x_nodes, w1, b1, gamma, beta, w2, b2, out):
         nc.scalar.activation(out=warm[:], in_=eps[:], func=ACT.Abs_reciprocal_sqrt)
         ident = consts.tile([P, P], F32)
         make_identity(nc, ident[:])
-        nc.scalar.dma_start(out=bias_rows[0:1, 0:HIDDEN], in_=b1.rearrange("(o n) -> o n", o=1))
-        nc.scalar.dma_start(out=bias_rows[0:1, HIDDEN:], in_=b2.rearrange("(o n) -> o n", o=1))
-        nc.scalar.dma_start(out=affine_rows[0:PASSES, :], in_=gamma.rearrange("(c n) -> c n", c=PASSES))
-        nc.scalar.dma_start(out=affine_rows[PASSES : 2 * PASSES, :], in_=beta.rearrange("(c n) -> c n", c=PASSES))
 
+        nc.sync.dma_start(out=bias_rows[0:1, 0:HIDDEN], in_=b1.rearrange("(o n) -> o n", o=1))
+        load_w1(1, 0)
+        load_x(0, 1)
         load_w1(0, 1)
         load_w1(1, 1)
-        load_x(1)
-        load_x(2)
+        nc.sync.dma_start(out=bias_rows[0:1, HIDDEN:], in_=b2.rearrange("(o n) -> o n", o=1))
+        nc.sync.dma_start(out=affine_rows[0:PASSES, :], in_=gamma.rearrange("(c n) -> c n", c=PASSES))
+        nc.sync.dma_start(out=affine_rows[PASSES : 2 * PASSES, :], in_=beta.rearrange("(c n) -> c n", c=PASSES))
+        for k in range(PAIR):
+            load_x(1, k)
         w2_planes = consts.tile([P, PASSES * PACK, FEATURES], BF16)
         for c in range(PASSES):
             nc.sync.dma_start(
                 out=w2_planes[:, PACK * c : PACK * (c + 1), :],
                 in_=w2[c * K_PASS : (c + 1) * K_PASS, :].rearrange("(p t) n -> p t n", t=PACK),
             )
-        for i in range(3, X_LOADS_AHEAD):
-            load_x(i)
+        for p in range(2, X_LOADS_AHEAD):
+            for k in range(PAIR):
+                load_x(p, k)
 
         def transpose_x(i):
-            if i >= N_TILES:
+            if i >= PAIR * N_PAIRS:
                 return
-            words = x_tiles[i][:].bitcast(F32)
-            xT_ps = psum.tile([P, PASSES, 2, P], F32, tag="xT", bufs=1)
+            p, k = divmod(i, PAIR)
+            words = x_tiles[p][:, k, :].bitcast(F32)
+            xT_ps = psum.tile([P, PASSES, 2, P], F32, tag="xT", bufs=2)
             for c in range(PASSES):
                 for u in range(2):
                     nc.tensor.transpose(
                         out=xT_ps[:, c, u, :], in_=words[:, 2 * P * c + u : 2 * P * (c + 1) : 2], identity=ident[:]
                     )
-            x_words[i] = xT_ps
+            x_banks[i] = xT_ps
 
         def copy_x(i):
-            if i >= N_TILES:
+            if i >= PAIR * N_PAIRS:
                 return
-            x_grouped = stage.tile([P, PASSES, P, 2], F32, tag="x_grouped", bufs=3, align_bytes=64)
-            nc.scalar.copy(out=x_grouped[:], in_=x_words[i][:].rearrange("q c u r -> q c r u"))
-            x_words[i] = x_grouped
+            p, k = divmod(i, PAIR)
+            if k == 0:
+                x_grouped = stage.tile([P, PAIR, PASSES, P, 2], F32, tag="x_grouped", bufs=2, align_bytes=64)
+                x_words[p] = x_grouped
+            nc.scalar.copy(out=x_words[p][:, k], in_=x_banks[i][:].rearrange("q c u r -> q c r u"))
 
-        def quantise_x(i):
-            if i >= N_TILES:
+        def quantise_x(p):
+            if not is_pair(p):
                 return
-            x_codes = stage.tile([P, PASSES, P], U32, tag="x_codes", bufs=3, align_bytes=64)
-            x_scales = stage.tile([P, PASSES, P], U8, tag="x_scales", bufs=3, align_bytes=64)
+            x_codes = stage.tile([P, PAIR, PASSES, P], U32, tag="x_codes", bufs=2, align_bytes=64)
+            x_scales = stage.tile([P, PAIR, PASSES, P], U8, tag="x_scales", bufs=2, align_bytes=64)
             nc.vector.quantize_mx(
-                out=x_codes[:].rearrange("q c r -> q (c r)").bitcast(FP8X4),
-                scales=x_scales[:].rearrange("q c r -> q (c r)"),
-                in_=x_words[i][:].rearrange("q c r u -> q (c r u)").bitcast(BF16),
+                out=x_codes[:].rearrange("q k c r -> q (k c r)").bitcast(FP8X4),
+                scales=x_scales[:].rearrange("q k c r -> q (k c r)"),
+                in_=x_words[p][:].rearrange("q k c r u -> q (k c r u)").bitcast(BF16),
             )
-            x_quantised[i] = (x_codes, x_scales)
+            x_quantised[p] = (x_codes, x_scales)
 
-        h_banks = {}
-
-        def layer1(i):
-            if i >= N_TILES:
+        def layer1(p, k, half):
+            if not is_pair(p):
                 return
-            x_codes, x_scales = x_quantised[i]
-            for half in range(HALVES):
-                cols = slice(half * BANK, (half + 1) * BANK)
-                h_ps = psum.tile([P, BANK], F32, tag="h", bufs=2)
-                for c in range(PASSES):
-                    nc.tensor.matmul_mx(
-                        out=h_ps[:],
-                        lhsT=x_codes[:, c, :].bitcast(FP8X4),
-                        lhsT_scale=x_scales[:, c, :],
-                        rhs=w1_codes[:, c, cols].bitcast(FP8X4),
-                        rhs_scale=w1_scales[:, c, cols],
-                        start=(c == 0),
-                        stop=(c == PASSES - 1),
-                    )
-                h_banks[i, half] = h_ps
-
-        def evacuate_h(i):
-            if i >= N_TILES:
-                return
-            biased = stage.tile([P, HIDDEN], F32, tag="normed", bufs=14)
-            sums = stage.tile([P, HALVES], F32, tag="sums", bufs=8)
-            for half in range(HALVES):
-                cols = slice(half * BANK, (half + 1) * BANK)
-                nc.vector.scalar_tensor_tensor(
-                    out=biased[:, cols].rearrange("r (t p) -> r t p", t=PACK),
-                    in0=h_banks[i, half][:].rearrange("r (p t) -> r t p", t=PACK),
-                    scalar=1.0,
-                    in1=b1_all[:, cols].rearrange("r (t p) -> r t p", t=PACK),
-                    op0=ALU.mult,
-                    op1=ALU.add,
-                    accum_out=sums[:, half : half + 1],
+            x_codes, x_scales = x_quantised[p]
+            cols = slice(half * BANK, (half + 1) * BANK)
+            h_ps = psum.tile([P, BANK], F32, tag="h", bufs=2)
+            for c in range(PASSES):
+                nc.tensor.matmul_mx(
+                    out=h_ps[:],
+                    lhsT=x_codes[:, k, c, :].bitcast(FP8X4),
+                    lhsT_scale=x_scales[:, k, c, :],
+                    rhs=w1_codes[:, c, cols].bitcast(FP8X4),
+                    rhs_scale=w1_scales[:, c, cols],
+                    start=(c == 0),
+                    stop=(c == PASSES - 1),
                 )
-            normed[i] = biased
-            row_sums[i] = sums
-
-        def mean(i):
-            if not 0 <= i < N_TILES:
-                return
-            negated = stage.tile([P, 1], F32, tag="minus_mean", bufs=8)
-            nc.vector.tensor_scalar(
-                out=negated[:],
-                in0=row_sums[i][:, 0:1],
-                scalar1=row_sums[i][:, 1:2],
-                scalar2=-1.0 / HIDDEN,
-                op0=ALU.add,
-                op1=ALU.mult,
+            if (p, k) not in normed:
+                biased = stage.tile([P, HIDDEN], F32, tag="normed", bufs=16)
+                normed[p, k] = biased
+            if p not in row_sums:
+                sums = stage.tile([P, HALVES, PAIR], F32, tag="sums", bufs=3)
+                row_sums[p] = sums
+            nc.vector.scalar_tensor_tensor(
+                out=normed[p, k][:, cols].rearrange("r (t p) -> r t p", t=PACK),
+                in0=h_ps[:].rearrange("r (p t) -> r t p", t=PACK),
+                scalar=1.0,
+                in1=b1_all[:, cols].rearrange("r (t p) -> r t p", t=PACK),
+                op0=ALU.mult,
+                op1=ALU.add,
+                accum_out=row_sums[p][:, half, k : k + 1],
             )
-            minus_mean[i] = negated
 
-        def square(i):
-            if not 0 <= i < N_TILES:
+        def mean(p):
+            if not is_pair(p):
                 return
+            total = stage.tile([P, PAIR], F32, tag="total", bufs=2)
+            nc.vector.tensor_tensor(out=total[:], in0=row_sums[p][:, 0, :], in1=row_sums[p][:, 1, :], op=ALU.add)
+            negated = stage.tile([P, PAIR], F32, tag="minus_mean", bufs=4)
+            nc.gpsimd.tensor_scalar(
+                out=negated[:], in0=total[:], scalar1=-1.0 / HIDDEN, scalar2=0.0, op0=ALU.mult, op1=ALU.add
+            )
+            minus_mean[p] = negated
+
+        def square(p, k):
+            if not is_pair(p):
+                return
+            if p not in squared:
+                sum_sq = stage.tile([P, PAIR], F32, tag="sum_sq", bufs=3)
+                squared[p] = sum_sq
             squares = stage.tile([P, HIDDEN], BF16, tag="squares", bufs=2)
-            sum_sq = stage.tile([P, 1], F32, tag="sum_sq", bufs=4)
             nc.scalar.activation(
                 out=squares[:],
-                in_=normed[i][:],
+                in_=normed[p, k][:],
                 func=ACT.Square,
-                bias=minus_mean[i][:, 0:1],
+                bias=minus_mean[p][:, k : k + 1],
                 scale=1.0,
-                accum_out=sum_sq[:, 0:1],
+                accum_out=squared[p][:, k : k + 1],
             )
-            squared[i] = sum_sq
 
-        def deviation(i):
-            if not 0 <= i < N_TILES:
+        def deviation(p):
+            if not is_pair(p):
                 return
-            inverse = stage.tile([P, 1], F32, tag="inv_std", bufs=6)
+            inverse = stage.tile([P, PAIR], F32, tag="inv_std", bufs=3)
             nc.scalar.activation(
                 out=inverse[:],
-                in_=squared[i][:],
+                in_=squared[p][:],
                 func=ACT.Abs_reciprocal_sqrt,
                 bias=eps[:, 0:1],
                 scale=1.0 / HIDDEN,
             )
-            inv_std[i] = inverse
+            inv_std[p] = inverse
 
-        def normalise(i):
-            if not 0 <= i < N_TILES:
+        def normalise(p):
+            if not is_pair(p):
                 return
-            gate = stage.tile([P, 1], F32, tag="gate", bufs=4)
-            nc.vector.tensor_copy(out=gate[:], in_=inv_std[i][:])
-            nc.gpsimd.tensor_scalar(
-                out=normed[i][:],
-                in0=normed[i][:],
-                scalar1=minus_mean[i][:, 0:1],
-                scalar2=gate[:, 0:1],
-                op0=ALU.add,
-                op1=ALU.mult,
-            )
+            last = p >= N_PAIRS - 1
+            if last:
+                engine, factor = nc.vector, inv_std[p]
+            else:
+                gate = stage.tile([P, PAIR], F32, tag="gate", bufs=3)
+                nc.vector.tensor_copy(out=gate[:], in_=inv_std[p][:])
+                engine, factor = nc.gpsimd, gate
+            for k in range(PAIR):
+                engine.tensor_scalar(
+                    out=normed[p, k][:],
+                    in0=normed[p, k][:],
+                    scalar1=minus_mean[p][:, k : k + 1],
+                    scalar2=factor[:, k : k + 1],
+                    op0=ALU.add,
+                    op1=ALU.mult,
+                )
 
         normedT = {}
 
-        def transpose_h(piece):
-            g, s = piece
-            size = GROUPS[g]
-            normedT_ps = psum.tile([P, MAX_GROUP * P], F32, tag="normedT", bufs=3)
-            for k in range(size):
-                nc.tensor.transpose(
-                    out=normedT_ps[:, k * P : (k + 1) * P],
-                    in_=normed[group_first[g] + k][:, s * P : (s + 1) * P],
-                    identity=ident[:],
+        def transpose_h(p, u):
+            if not is_pair(p):
+                return
+            normedT_ps = psum.tile([P, 2, PAIR_TOKENS], F32, tag="normedT", bufs=2)
+            for v in range(2):
+                s = 2 * u + v
+                for k in range(PAIR):
+                    nc.tensor.transpose(
+                        out=normedT_ps[:, v, k * P : (k + 1) * P],
+                        in_=normed[p, k][:, s * P : (s + 1) * P],
+                        identity=ident[:],
+                    )
+            normedT[p, u] = normedT_ps
+
+        def relu(p, u):
+            if not is_pair(p):
+                return
+            if u == 0:
+                planes = stage.tile([P, SLICES, PAIR_TOKENS], BF16, tag="r_planes", bufs=3)
+                r_planes[p] = planes
+            for v in range(2):
+                s = 2 * u + v
+                c, t = divmod(s, PACK)
+                nc.scalar.activation(
+                    out=r_planes[p][:, s, :],
+                    in_=normedT[p, u][:, v, :],
+                    func=ACT.Relu,
+                    bias=affine_cols[:, t, PASSES + c : PASSES + c + 1],
+                    scale=affine_cols[:, t, c : c + 1],
                 )
-            normedT[piece] = normedT_ps
 
-        def relu(piece):
-            g, s = piece
-            if s == 0:
-                planes = stage.tile([P, SLICES, MAX_GROUP * P], BF16, tag="r_planes", bufs=2)
-                r_planes[g] = planes
-            width = GROUPS[g] * P
-            c, t = divmod(s, PACK)
-            nc.scalar.activation(
-                out=r_planes[g][:, s, 0:width],
-                in_=normedT[piece][:, 0:width],
-                func=ACT.Relu,
-                bias=affine_cols[:, t, PASSES + c : PASSES + c + 1],
-                scale=affine_cols[:, t, c : c + 1],
-            )
+        def regroup_r(p, c):
+            if not is_pair(p):
+                return
+            grouped = stage.tile([P, PAIR_TOKENS, PACK], BF16, tag="r_grouped", bufs=4, align_bytes=64)
+            regroup(nc.vector.tensor_copy, grouped[:], r_planes[p][:, PACK * c : PACK * (c + 1), :])
+            r_grouped[p, c] = grouped
 
-        def regroup_r(piece):
-            g, c = piece
-            width = GROUPS[g] * P
-            grouped = stage.tile([P, MAX_GROUP * P, PACK], BF16, tag="r_grouped", bufs=2, align_bytes=64)
-            regroup(nc.vector.tensor_copy, grouped[:, 0:width, :], r_planes[g][:, PACK * c : PACK * (c + 1), 0:width])
-            r_grouped[piece] = grouped
-
-        def quantise_r(piece):
-            g, c = piece
-            width = GROUPS[g] * P
-            if c == 0:
-                codes = stage.tile([P, PASSES, MAX_GROUP * P], U32, tag="r_codes", bufs=2, align_bytes=64)
-                scales = stage.tile([P, PASSES, MAX_GROUP * P], U8, tag="r_scales", bufs=2, align_bytes=64)
-                r_quantised[g] = (codes, scales)
-            r_codes, r_scales = r_quantised[g]
+        def quantise_r(p, c):
+            if not is_pair(p):
+                return
+            codes = stage.tile([P, PAIR_TOKENS], U32, tag="r_codes", bufs=6, align_bytes=64)
+            scales = stage.tile([P, PAIR_TOKENS], U8, tag="r_scales", bufs=6, align_bytes=64)
             nc.vector.quantize_mx(
-                out=r_codes[:, c, 0:width].bitcast(FP8X4),
-                scales=r_scales[:, c, 0:width],
-                in_=r_grouped[piece][:, 0:width, :].rearrange("p n t -> p (n t)"),
+                out=codes[:].bitcast(FP8X4),
+                scales=scales[:],
+                in_=r_grouped[p, c][:].rearrange("p n t -> p (n t)"),
             )
+            r_quantised[p, c] = (codes, scales)
 
-        x1_banks = {}
-
-        def layer2(piece):
-            g, pair = piece
-            r_codes, r_scales = r_quantised[g]
-            x1_ps = psum.tile([P, 2, FEATURES], F32, tag="x1")
-            for j in range(min(2, GROUPS[g] - 2 * pair)):
-                tokens = slice((2 * pair + j) * P, (2 * pair + j + 1) * P)
+        def layer2(p):
+            if not is_pair(p):
+                return
+            x1_ps = psum.tile([P, PAIR, FEATURES], F32, tag="x1")
+            for k in range(PAIR):
                 for c in range(PASSES):
+                    codes, scales = r_quantised[p, c]
                     nc.tensor.matmul_mx(
-                        out=x1_ps[:, j, :],
-                        lhsT=r_codes[:, c, tokens].bitcast(FP8X4),
-                        lhsT_scale=r_scales[:, c, tokens],
+                        out=x1_ps[:, k, :],
+                        lhsT=codes[:, k * P : (k + 1) * P].bitcast(FP8X4),
+                        lhsT_scale=scales[:, k * P : (k + 1) * P],
                         rhs=w2_codes[:, c, :].bitcast(FP8X4),
                         rhs_scale=w2_scales[:, c, :],
                         start=(c == 0),
                         stop=(c == PASSES - 1),
                     )
-            x1_banks[piece] = x1_ps
+            x1_banks[p] = x1_ps
 
-        def evacuate_x1(piece):
-            g, pair = piece
-            size = GROUPS[g]
-            if pair == 0:
-                x1_sb = stage.tile([P, MAX_GROUP, FEATURES], F32, tag="x1_sb", bufs=3)
-                x1_tiles[g] = x1_sb
-            count = min(2, size - 2 * pair)
+        def evacuate_x1(p):
+            if not is_pair(p):
+                return
+            x1_sb = stage.tile([P, PAIR, FEATURES], F32, tag="x1_sb", bufs=5)
             nc.vector.tensor_tensor(
-                out=x1_tiles[g][:, 2 * pair : 2 * pair + count, :],
-                in0=x1_banks[piece][:, 0:count, :],
-                in1=b2_all.unsqueeze(1).to_broadcast([P, count, FEATURES]),
+                out=x1_sb[:],
+                in0=x1_banks[p][:],
+                in1=b2_all.unsqueeze(1).to_broadcast([P, PAIR, FEATURES]),
                 op=ALU.add,
             )
-            if 2 * pair + count == size:
-                rows = slice(group_first[g] * P, (group_first[g] + size) * P)
-                nc.sync.dma_start(
-                    out=out_rows[rows, 0:FEATURES].rearrange("(g p) f -> p g f", p=P),
-                    in_=x1_tiles[g][:, 0:size, :],
-                )
+            x1_tiles[p] = x1_sb
+            rows = slice(p * PAIR_TOKENS, (p + 1) * PAIR_TOKENS)
+            nc.sync.dma_start(out=out_rows[rows, 0:FEATURES].rearrange("(k p) f -> p k f", p=P), in_=x1_sb[:])
 
-        pooled_banks = {}
-
-        def transpose_x1(piece):
-            g, pair = piece
-            x1T_ps = psum.tile([P, FEATURES // P, 2 * P], F32, tag="pooled")
-            for s in range(FEATURES // P):
-                for j in range(min(2, GROUPS[g] - 2 * pair)):
+        def transpose_x1(p):
+            if not is_pair(p):
+                return
+            x1T_ps = psum.tile([P, FEATURE_SLICES, PAIR_TOKENS], F32, tag="pooled")
+            for s in range(FEATURE_SLICES):
+                for k in range(PAIR):
                     nc.tensor.transpose(
-                        out=x1T_ps[:, s, j * P : (j + 1) * P],
-                        in_=x1_tiles[g][:, 2 * pair + j, s * P : (s + 1) * P],
+                        out=x1T_ps[:, s, k * P : (k + 1) * P],
+                        in_=x1_tiles[p][:, k, s * P : (s + 1) * P],
                         identity=ident[:],
                     )
-            pooled_banks[piece] = x1T_ps
+            pooled_banks[p] = x1T_ps
 
-        def pool(piece):
-            g, pair = piece
-            size = GROUPS[g]
-            lines = size * P // NODES
-            if pair == 0:
-                maxima = stage.tile([P, FEATURES // P, MAX_GROUP * P // NODES], F32, tag="line_max", bufs=2)
-                line_max[g] = maxima
-            count = min(2, size - 2 * pair)
-            first = 2 * pair * P // NODES
+        def pool(p):
+            if not is_pair(p):
+                return
+            batch, member = divmod(p, BATCH)
+            if member == 0:
+                maxima = stage.tile([P, FEATURE_SLICES, BATCH_LINES], F32, tag="line_max", bufs=2)
+                line_max[batch] = maxima
+            lines = BATCH_LINES // BATCH
             nc.vector.tensor_reduce(
-                out=line_max[g][:, :, first : first + count * P // NODES],
-                in_=pooled_banks[piece][:, :, 0 : count * P].rearrange("f s (b l) -> f s b l", l=NODES),
+                out=line_max[batch][:, :, member * lines : (member + 1) * lines],
+                in_=pooled_banks[p][:].rearrange("f s (b l) -> f s b l", l=NODES),
                 axis=AXIS.X,
                 op=ALU.max,
             )
 
-        def repeat(g):
-            lines = GROUPS[g] * P // NODES
-            copies = P // lines
-            rep = stage.tile([P, FEATURES // P, P], F32, tag="repeated", bufs=2)
+        def repeat(p):
+            if not is_pair(p) or p % BATCH != BATCH - 1:
+                return
+            batch = p // BATCH
+            copies = stage.tile([P, FEATURE_SLICES, BATCH_LINES, COPIES], F32, tag="repeated", bufs=2)
             nc.scalar.copy(
-                out=rep[:].rearrange("f s (b i) -> f s b i", i=copies),
-                in_=line_max[g][:, :, 0:lines].unsqueeze(3).to_broadcast([P, FEATURES // P, lines, copies]),
+                out=copies[:],
+                in_=line_max[batch][:].unsqueeze(3).to_broadcast([P, FEATURE_SLICES, BATCH_LINES, COPIES]),
             )
-            repeated[g] = rep
+            repeated[batch] = copies
 
-        def store_pooled(g):
-            size = GROUPS[g]
+        def store_pooled(p):
+            if not is_pair(p) or p % BATCH != BATCH - 1:
+                return
+            batch = p // BATCH
             x2_ps = psum.tile([P, FEATURES], F32, tag="pooled")
-            for s in range(FEATURES // P):
+            for s in range(FEATURE_SLICES):
                 nc.tensor.transpose(
-                    out=x2_ps[:, s * P : (s + 1) * P], in_=repeated[g][:, s, :], identity=ident[:]
+                    out=x2_ps[:, s * P : (s + 1) * P],
+                    in_=repeated[batch][:, s, :, :].rearrange("f b i -> f (b i)"),
+                    identity=ident[:],
                 )
             x2_sb = stage.tile([P, FEATURES], F32, tag="x2_sb", bufs=2)
             nc.scalar.copy(out=x2_sb[:], in_=x2_ps[:])
-            rows = slice(group_first[g] * P, (group_first[g] + size) * P)
+            rows = slice(batch * BATCH_TOKENS, (batch + 1) * BATCH_TOKENS)
+            nodes_each = NODES // COPIES
             nc.sync.dma_start(
-                out=out_rows[rows, FEATURES : 2 * FEATURES].rearrange("(p m) f -> p m f", m=size),
-                in_=x2_sb[:].unsqueeze(1).to_broadcast([P, size, FEATURES]),
+                out=out_rows[rows, FEATURES : 2 * FEATURES].rearrange("(p m) f -> p m f", m=nodes_each),
+                in_=x2_sb[:].unsqueeze(1).to_broadcast([P, nodes_each, FEATURES]),
             )
 
         bias_all = consts.tile([P, HIDDEN + FEATURES], BF16)
@@ -452,10 +429,9 @@ def tile_sub_graph_pa_t_kernel(tc, x_nodes, w1, b1, gamma, beta, w2, b2, out):
 
         def regroup_w1(c, half):
             grouped = stage.tile([P, BANK, PACK], BF16, tag="w1_grouped", bufs=2, align_bytes=64)
-            split = 320
             planes = w1_planes[c, half]
-            regroup(nc.vector.tensor_copy, grouped[:, 0:split, :], planes[:, :, 0:split])
-            regroup(nc.scalar.copy, grouped[:, split:BANK, :], planes[:, :, split:BANK])
+            regroup(nc.vector.tensor_copy, grouped[:, 0:320, :], planes[:, :, 0:320])
+            regroup(nc.scalar.copy, grouped[:, 320:BANK, :], planes[:, :, 320:BANK])
             w1_grouped[c, half] = grouped
 
         def quantise_w1(c, half):
@@ -472,16 +448,15 @@ def tile_sub_graph_pa_t_kernel(tc, x_nodes, w1, b1, gamma, beta, w2, b2, out):
         spread_bias(0)
         regroup_w1(1, 0)
         quantise_w1(0, 0)
-        quantise_x(0)
+        transpose_x(1)
+        copy_x(1)
         spread_bias(BANK)
         quantise_w1(1, 0)
+        quantise_x(0)
         regroup_w1(0, 1)
         regroup_w1(1, 1)
         quantise_w1(0, 1)
         quantise_w1(1, 1)
-        for i in range(1, X_AHEAD):
-            transpose_x(i)
-            copy_x(i)
 
         affine_f32 = consts.tile([P, PACK, P], F32)
         affine_cols = consts.tile([P, PACK, 2 * PASSES], F32)
@@ -496,54 +471,47 @@ def tile_sub_graph_pa_t_kernel(tc, x_nodes, w1, b1, gamma, beta, w2, b2, out):
                 nc.tensor.transpose(out=affine_ps[:, t, :], in_=affine_f32[:, t, :], identity=ident[:])
             nc.vector.tensor_copy(out=affine_cols[:], in_=affine_ps[:, :, 0 : 2 * PASSES])
 
-        for step in range(last_step + 1):
-
-            def due(stage_name):
-                return table.get((step, stage_name), [])
-
-            load_x(step + X_LOADS_AHEAD)
-            pieces = due("relu")
+        for step in range(N_STEPS):
+            for k in range(PAIR):
+                load_x(step + X_LOADS_AHEAD, k)
+            transpose_x(2 * (step + 1))
+            transpose_x(2 * (step + 1) + 1)
+            transpose_h(step - RELU, 0)
+            transpose_h(step - RELU, 1)
+            copy_x(2 * (step + 1))
+            copy_x(2 * (step + 1) + 1)
+            relu(step - RELU, 0)
+            relu(step - RELU, 1)
+            regroup_r(step - REGROUP, 0)
+            regroup_r(step - REGROUP, 1)
+            quantise_r(step - QUANT, 0)
+            quantise_r(step - QUANT, 1)
+            normalise(step - NORM)
+            square(step - 1, 0)
+            square(step - 1, 1)
+            layer1(step, 0, 0)
+            layer1(step, 0, 1)
+            repeat(step - REPEAT)
+            transpose_x1(step - POOL)
+            transpose_h(step - RELU, 2)
+            pool(step - POOL)
+            layer1(step, 1, 0)
+            layer1(step, 1, 1)
+            relu(step - RELU, 2)
+            layer2(step - LAYER2)
+            transpose_h(step - RELU, 3)
+            relu(step - RELU, 3)
             quantise_x(step + 1)
-            for piece in due("quantise"):
-                quantise_r(piece)
-            for piece in due("regroup"):
-                regroup_r(piece)
-            normalise(step - 2)
-            mean(step - 1)
-            transpose_x(step + X_AHEAD)
-            for piece in pieces[0:2]:
-                transpose_h(piece)
-            for piece in due("pool"):
-                transpose_x1(piece)
-            layer1(step)
-            for piece in due("layer2"):
-                layer2(piece)
-            for piece in pieces[0:1]:
-                relu(piece)
-            for g in due("repeat"):
-                repeat(g)
-            copy_x(step + X_AHEAD)
-            square(step - 1)
-            for g in due("store"):
-                store_pooled(g)
-            for piece in pieces[1:2]:
-                relu(piece)
-            for piece in pieces[2:]:
-                transpose_h(piece)
-                relu(piece)
+            evacuate_x1(step - X1_OUT)
+            store_pooled(step - STORE)
             deviation(step - 1)
-            for piece in due("pool"):
-                pool(piece)
-            evacuate_h(step)
-            for piece in due("layer2"):
-                evacuate_x1(piece)
+            mean(step)
             if step == 0:
                 spread_bias(2 * BANK)
-            if step == 1:
                 load_affine()
+            if step == 1:
                 for c in range(PASSES):
                     regroup(nc.vector.tensor_copy, w2_grouped[:, c, :, :], w2_planes[:, PACK * c : PACK * (c + 1), :])
-            if step == 2:
                 nc.vector.quantize_mx(
                     out=w2_codes[:].rearrange("p c n -> p (c n)").bitcast(FP8X4),
                     scales=w2_scales[:].rearrange("p c n -> p (c n)"),

@@ -32,6 +32,7 @@ PAIR_TOKENS = PAIR * P
 N_PAIRS = TOKENS // PAIR_TOKENS
 HALVES = HIDDEN // BANK
 FEATURE_SLICES = FEATURES // P
+UNITS = SLICES // 2
 
 BATCH = 2
 BATCH_LINES = BATCH * PAIR_TOKENS // NODES
@@ -41,13 +42,9 @@ BATCH_TOKENS = BATCH * PAIR_TOKENS
 NORM = 2
 RELU = 3
 REGROUP = 4
-QUANT = 4
-LAYER2 = 4
-X1_OUT = 4
-POOL = 5
-REPEAT = 6
-STORE = 6
-N_STEPS = N_PAIRS + STORE
+LAYER2 = 5
+POOL = 6
+STORE = 7
 X_LOADS_AHEAD = 4
 
 
@@ -69,9 +66,15 @@ def tile_sub_graph_pa_t_kernel(tc, x_nodes, w1, b1, gamma, beta, w2, b2, out):
         psum = ctx.enter_context(tc.psum_pool(name="psum", bufs=1))
         ctx.enter_context(tc.manual_schedule())
 
+        bank_bufs = {"xT": 2, "h": 2, "normedT": 2, "x1": 1, "pooled": 1}
+
+        def bank(shape, tag, dtype=F32):
+            tile = psum.tile(shape, dtype, tag=tag, bufs=bank_bufs[tag])
+            return tile
+
         x_tiles, x_banks, x_words, x_quantised = {}, {}, {}, {}
-        normed, row_sums, minus_mean, squared, inv_std = {}, {}, {}, {}, {}
-        h_banks, r_planes, r_grouped, r_quantised = {}, {}, {}, {}
+        h_banks, normed, row_sums, minus_mean, squared, inv_std = {}, {}, {}, {}, {}, {}
+        normedT, r_planes, r_grouped, r_quantised = {}, {}, {}, {}
         x1_banks, x1_tiles, pooled_banks, line_max, repeated = {}, {}, {}, {}, {}
 
         def is_pair(p):
@@ -110,6 +113,8 @@ def tile_sub_graph_pa_t_kernel(tc, x_nodes, w1, b1, gamma, beta, w2, b2, out):
         nc.scalar.activation(out=warm[:], in_=eps[:], func=ACT.Abs_reciprocal_sqrt)
         ident = consts.tile([P, P], F32)
         make_identity(nc, ident[:])
+        ident_bf16 = consts.tile([P, P], BF16)
+        nc.gpsimd.tensor_copy(out=ident_bf16[:], in_=ident[:])
 
         nc.sync.dma_start(out=bias_rows[0:1, 0:HIDDEN], in_=b1.rearrange("(o n) -> o n", o=1))
         load_w1(1, 0)
@@ -131,27 +136,40 @@ def tile_sub_graph_pa_t_kernel(tc, x_nodes, w1, b1, gamma, beta, w2, b2, out):
             for k in range(PAIR):
                 load_x(p, k)
 
-        def transpose_x(i):
-            if i >= PAIR * N_PAIRS:
+        def transpose_x(p, k, tag="xT"):
+            if not is_pair(p):
                 return
-            p, k = divmod(i, PAIR)
             words = x_tiles[p][:, k, :].bitcast(F32)
-            xT_ps = psum.tile([P, PASSES, 2, P], F32, tag="xT", bufs=2)
+            xT_ps = bank([P, PASSES, 2, P], tag)
             for c in range(PASSES):
                 for u in range(2):
                     nc.tensor.transpose(
                         out=xT_ps[:, c, u, :], in_=words[:, 2 * P * c + u : 2 * P * (c + 1) : 2], identity=ident[:]
                     )
-            x_banks[i] = xT_ps
+            x_banks[p, k] = xT_ps
 
-        def copy_x(i):
-            if i >= PAIR * N_PAIRS:
+        def copy_x(p, k):
+            if not is_pair(p):
                 return
-            p, k = divmod(i, PAIR)
-            if k == 0:
-                x_grouped = stage.tile([P, PAIR, PASSES, P, 2], F32, tag="x_grouped", bufs=2, align_bytes=64)
-                x_words[p] = x_grouped
-            nc.scalar.copy(out=x_words[p][:, k], in_=x_banks[i][:].rearrange("q c u r -> q c r u"))
+            if p == 0:
+                words = stage.tile([P, PASSES, P, 2], F32, tag="x_grouped_first", bufs=2, align_bytes=64)
+                x_words[p, k] = words[:]
+            else:
+                if k == 0:
+                    x_pair = stage.tile([P, PAIR, PASSES, P, 2], F32, tag="x_grouped", bufs=2, align_bytes=64)
+                    x_words[p] = x_pair
+                x_words[p, k] = x_words[p][:, k]
+            nc.scalar.copy(out=x_words[p, k], in_=x_banks[p, k][:].rearrange("q c u r -> q c r u"))
+
+        def quantise_x_tile(p, k):
+            x_codes = stage.tile([P, PASSES, P], U32, tag="x_codes_first", bufs=2, align_bytes=64)
+            x_scales = stage.tile([P, PASSES, P], U8, tag="x_scales_first", bufs=2, align_bytes=64)
+            nc.vector.quantize_mx(
+                out=x_codes[:].rearrange("q c r -> q (c r)").bitcast(FP8X4),
+                scales=x_scales[:].rearrange("q c r -> q (c r)"),
+                in_=x_words[p, k].rearrange("q c r u -> q (c r u)").bitcast(BF16),
+            )
+            x_quantised[p, k] = (x_codes[:], x_scales[:])
 
         def quantise_x(p):
             if not is_pair(p):
@@ -163,24 +181,31 @@ def tile_sub_graph_pa_t_kernel(tc, x_nodes, w1, b1, gamma, beta, w2, b2, out):
                 scales=x_scales[:].rearrange("q k c r -> q (k c r)"),
                 in_=x_words[p][:].rearrange("q k c r u -> q (k c r u)").bitcast(BF16),
             )
-            x_quantised[p] = (x_codes, x_scales)
+            for k in range(PAIR):
+                x_quantised[p, k] = (x_codes[:, k], x_scales[:, k])
 
-        def layer1(p, k, half):
+        def layer1(p, k, half, tag="h"):
             if not is_pair(p):
                 return
-            x_codes, x_scales = x_quantised[p]
+            x_codes, x_scales = x_quantised[p, k]
             cols = slice(half * BANK, (half + 1) * BANK)
-            h_ps = psum.tile([P, BANK], F32, tag="h", bufs=2)
+            h_ps = bank([P, BANK], tag)
             for c in range(PASSES):
                 nc.tensor.matmul_mx(
                     out=h_ps[:],
-                    lhsT=x_codes[:, k, c, :].bitcast(FP8X4),
-                    lhsT_scale=x_scales[:, k, c, :],
+                    lhsT=x_codes[:, c, :].bitcast(FP8X4),
+                    lhsT_scale=x_scales[:, c, :],
                     rhs=w1_codes[:, c, cols].bitcast(FP8X4),
                     rhs_scale=w1_scales[:, c, cols],
                     start=(c == 0),
                     stop=(c == PASSES - 1),
                 )
+            h_banks[p, k, half] = h_ps
+
+        def add_b1(p, k, half):
+            if not is_pair(p):
+                return
+            cols = slice(half * BANK, (half + 1) * BANK)
             if (p, k) not in normed:
                 biased = stage.tile([P, HIDDEN], F32, tag="normed", bufs=16)
                 normed[p, k] = biased
@@ -189,7 +214,7 @@ def tile_sub_graph_pa_t_kernel(tc, x_nodes, w1, b1, gamma, beta, w2, b2, out):
                 row_sums[p] = sums
             nc.vector.scalar_tensor_tensor(
                 out=normed[p, k][:, cols].rearrange("r (t p) -> r t p", t=PACK),
-                in0=h_ps[:].rearrange("r (p t) -> r t p", t=PACK),
+                in0=h_banks[p, k, half][:].rearrange("r (p t) -> r t p", t=PACK),
                 scalar=1.0,
                 in1=b1_all[:, cols].rearrange("r (t p) -> r t p", t=PACK),
                 op0=ALU.mult,
@@ -200,12 +225,16 @@ def tile_sub_graph_pa_t_kernel(tc, x_nodes, w1, b1, gamma, beta, w2, b2, out):
         def mean(p):
             if not is_pair(p):
                 return
-            total = stage.tile([P, PAIR], F32, tag="total", bufs=2)
-            nc.vector.tensor_tensor(out=total[:], in0=row_sums[p][:, 0, :], in1=row_sums[p][:, 1, :], op=ALU.add)
             negated = stage.tile([P, PAIR], F32, tag="minus_mean", bufs=4)
-            nc.gpsimd.tensor_scalar(
-                out=negated[:], in0=total[:], scalar1=-1.0 / HIDDEN, scalar2=0.0, op0=ALU.mult, op1=ALU.add
-            )
+            for k in range(PAIR):
+                nc.vector.tensor_scalar(
+                    out=negated[:, k : k + 1],
+                    in0=row_sums[p][:, 0, k : k + 1],
+                    scalar1=row_sums[p][:, 1, k : k + 1],
+                    scalar2=-1.0 / HIDDEN,
+                    op0=ALU.add,
+                    op1=ALU.mult,
+                )
             minus_mean[p] = negated
 
         def square(p, k):
@@ -237,11 +266,10 @@ def tile_sub_graph_pa_t_kernel(tc, x_nodes, w1, b1, gamma, beta, w2, b2, out):
             )
             inv_std[p] = inverse
 
-        def normalise(p):
+        def normalise(p, on_vector=False):
             if not is_pair(p):
                 return
-            last = p >= N_PAIRS - 1
-            if last:
+            if on_vector:
                 engine, factor = nc.vector, inv_std[p]
             else:
                 gate = stage.tile([P, PAIR], F32, tag="gate", bufs=3)
@@ -257,12 +285,10 @@ def tile_sub_graph_pa_t_kernel(tc, x_nodes, w1, b1, gamma, beta, w2, b2, out):
                     op1=ALU.mult,
                 )
 
-        normedT = {}
-
-        def transpose_h(p, u):
+        def transpose_h(p, u, tag="normedT"):
             if not is_pair(p):
                 return
-            normedT_ps = psum.tile([P, 2, PAIR_TOKENS], F32, tag="normedT", bufs=2)
+            normedT_ps = bank([P, 2, PAIR_TOKENS], tag)
             for v in range(2):
                 s = 2 * u + v
                 for k in range(PAIR):
@@ -286,8 +312,8 @@ def tile_sub_graph_pa_t_kernel(tc, x_nodes, w1, b1, gamma, beta, w2, b2, out):
                     out=r_planes[p][:, s, :],
                     in_=normedT[p, u][:, v, :],
                     func=ACT.Relu,
-                    bias=affine_cols[:, t, PASSES + c : PASSES + c + 1],
-                    scale=affine_cols[:, t, c : c + 1],
+                    bias=columns[:, t, PASSES + c : PASSES + c + 1],
+                    scale=columns[:, t, c : c + 1],
                 )
 
         def regroup_r(p, c):
@@ -309,10 +335,10 @@ def tile_sub_graph_pa_t_kernel(tc, x_nodes, w1, b1, gamma, beta, w2, b2, out):
             )
             r_quantised[p, c] = (codes, scales)
 
-        def layer2(p):
+        def layer2(p, tag="x1"):
             if not is_pair(p):
                 return
-            x1_ps = psum.tile([P, PAIR, FEATURES], F32, tag="x1")
+            x1_ps = bank([P, PAIR, FEATURES], tag)
             for k in range(PAIR):
                 for c in range(PASSES):
                     codes, scales = r_quantised[p, c]
@@ -327,7 +353,7 @@ def tile_sub_graph_pa_t_kernel(tc, x_nodes, w1, b1, gamma, beta, w2, b2, out):
                     )
             x1_banks[p] = x1_ps
 
-        def evacuate_x1(p):
+        def add_b2(p):
             if not is_pair(p):
                 return
             x1_sb = stage.tile([P, PAIR, FEATURES], F32, tag="x1_sb", bufs=5)
@@ -341,16 +367,32 @@ def tile_sub_graph_pa_t_kernel(tc, x_nodes, w1, b1, gamma, beta, w2, b2, out):
             rows = slice(p * PAIR_TOKENS, (p + 1) * PAIR_TOKENS)
             nc.sync.dma_start(out=out_rows[rows, 0:FEATURES].rearrange("(k p) f -> p k f", p=P), in_=x1_sb[:])
 
-        def transpose_x1(p):
+        def transpose_x1(p, tag="pooled"):
             if not is_pair(p):
                 return
-            x1T_ps = psum.tile([P, FEATURE_SLICES, PAIR_TOKENS], F32, tag="pooled")
+            x1T_ps = bank([P, FEATURE_SLICES, PAIR_TOKENS], tag)
             for s in range(FEATURE_SLICES):
                 for k in range(PAIR):
                     nc.tensor.transpose(
                         out=x1T_ps[:, s, k * P : (k + 1) * P],
                         in_=x1_tiles[p][:, k, s * P : (s + 1) * P],
                         identity=ident[:],
+                    )
+            pooled_banks[p] = x1T_ps
+
+        def layer2_transposed(p, tag):
+            x1T_ps = bank([P, FEATURE_SLICES, PAIR_TOKENS], tag)
+            for s in range(FEATURE_SLICES):
+                for c in range(PASSES):
+                    codes, scales = r_quantised[p, c]
+                    nc.tensor.matmul_mx(
+                        out=x1T_ps[:, s, :],
+                        lhsT=w2_codes[:, c, s * P : (s + 1) * P].bitcast(FP8X4),
+                        lhsT_scale=w2_scales[:, c, s * P : (s + 1) * P],
+                        rhs=codes[:].bitcast(FP8X4),
+                        rhs_scale=scales[:],
+                        start=(c == 0),
+                        stop=(c == PASSES - 1),
                     )
             pooled_banks[p] = x1T_ps
 
@@ -369,22 +411,32 @@ def tile_sub_graph_pa_t_kernel(tc, x_nodes, w1, b1, gamma, beta, w2, b2, out):
                 op=ALU.max,
             )
 
-        def repeat(p):
+        def repeat(p, biased=True):
             if not is_pair(p) or p % BATCH != BATCH - 1:
                 return
             batch = p // BATCH
             copies = stage.tile([P, FEATURE_SLICES, BATCH_LINES, COPIES], F32, tag="repeated", bufs=2)
-            nc.scalar.copy(
-                out=copies[:],
-                in_=line_max[batch][:].unsqueeze(3).to_broadcast([P, FEATURE_SLICES, BATCH_LINES, COPIES]),
-            )
+            if biased:
+                nc.scalar.copy(
+                    out=copies[:],
+                    in_=line_max[batch][:].unsqueeze(3).to_broadcast([P, FEATURE_SLICES, BATCH_LINES, COPIES]),
+                )
+            else:
+                for s in range(FEATURE_SLICES):
+                    nc.scalar.activation(
+                        out=copies[:, s],
+                        in_=line_max[batch][:, s].unsqueeze(2).to_broadcast([P, BATCH_LINES, COPIES]),
+                        func=ACT.Identity,
+                        bias=columns[:, PACK + s, 0:1],
+                        scale=1.0,
+                    )
             repeated[batch] = copies
 
-        def store_pooled(p):
+        def store_pooled(p, tag="pooled"):
             if not is_pair(p) or p % BATCH != BATCH - 1:
                 return
             batch = p // BATCH
-            x2_ps = psum.tile([P, FEATURES], F32, tag="pooled")
+            x2_ps = bank([P, FEATURES], tag)
             for s in range(FEATURE_SLICES):
                 nc.tensor.transpose(
                     out=x2_ps[:, s * P : (s + 1) * P],
@@ -401,10 +453,12 @@ def tile_sub_graph_pa_t_kernel(tc, x_nodes, w1, b1, gamma, beta, w2, b2, out):
             )
 
         bias_all = consts.tile([P, HIDDEN + FEATURES], BF16)
+        b1_all = bias_all[:, 0:HIDDEN]
+        b2_all = bias_all[:, HIDDEN:]
 
-        def spread_bias(first):
+        def spread_bias(first, tag):
             width = min(BANK, HIDDEN + FEATURES - first)
-            bias_ps = psum.tile([P, BANK], F32, tag="h", bufs=2)
+            bias_ps = bank([P, BANK], tag)
             nc.tensor.matmul(
                 out=bias_ps[:, 0:width],
                 lhsT=ones[:],
@@ -420,18 +474,15 @@ def tile_sub_graph_pa_t_kernel(tc, x_nodes, w1, b1, gamma, beta, w2, b2, out):
             else:
                 nc.scalar.copy(out=bias_all[:, first : first + width], in_=bias_ps[:, 0:width])
 
-        b1_all = bias_all[:, 0:HIDDEN]
-        b2_all = bias_all[:, HIDDEN:]
-
         w1_codes = consts.tile([P, PASSES, HIDDEN], U32, align_bytes=64)
         w1_scales = consts.tile([P, PASSES, HIDDEN], U8, align_bytes=64)
         w1_grouped = {}
 
-        def regroup_w1(c, half):
+        def regroup_w1(c, half, on_vector):
             grouped = stage.tile([P, BANK, PACK], BF16, tag="w1_grouped", bufs=2, align_bytes=64)
             planes = w1_planes[c, half]
-            regroup(nc.vector.tensor_copy, grouped[:, 0:320, :], planes[:, :, 0:320])
-            regroup(nc.scalar.copy, grouped[:, 320:BANK, :], planes[:, :, 320:BANK])
+            regroup(nc.vector.tensor_copy, grouped[:, 0:on_vector, :], planes[:, :, 0:on_vector])
+            regroup(nc.scalar.copy, grouped[:, on_vector:BANK, :], planes[:, :, on_vector:BANK])
             w1_grouped[c, half] = grouped
 
         def quantise_w1(c, half):
@@ -442,78 +493,205 @@ def tile_sub_graph_pa_t_kernel(tc, x_nodes, w1, b1, gamma, beta, w2, b2, out):
                 in_=w1_grouped[c, half][:].rearrange("p n t -> p (n t)"),
             )
 
-        transpose_x(0)
-        regroup_w1(0, 0)
-        copy_x(0)
-        spread_bias(0)
-        regroup_w1(1, 0)
-        quantise_w1(0, 0)
-        transpose_x(1)
-        copy_x(1)
-        spread_bias(BANK)
-        quantise_w1(1, 0)
-        quantise_x(0)
-        regroup_w1(0, 1)
-        regroup_w1(1, 1)
-        quantise_w1(0, 1)
-        quantise_w1(1, 1)
-
-        affine_f32 = consts.tile([P, PACK, P], F32)
-        affine_cols = consts.tile([P, PACK, 2 * PASSES], F32)
         w2_grouped = consts.tile([P, PASSES, FEATURES, PACK], BF16, align_bytes=64)
         w2_codes = consts.tile([P, PASSES, FEATURES], U32, align_bytes=64)
         w2_scales = consts.tile([P, PASSES, FEATURES], U8, align_bytes=64)
 
-        def load_affine():
-            nc.vector.tensor_copy(out=affine_f32[:], in_=affine_rows[:].rearrange("r (p t) -> r t p", t=PACK))
-            affine_ps = psum.tile([P, PACK, P], F32, tag="pooled")
-            for t in range(PACK):
-                nc.tensor.transpose(out=affine_ps[:, t, :], in_=affine_f32[:, t, :], identity=ident[:])
-            nc.vector.tensor_copy(out=affine_cols[:], in_=affine_ps[:, :, 0 : 2 * PASSES])
+        def regroup_w2():
+            for c in range(PASSES):
+                regroup(nc.scalar.copy, w2_grouped[:, c, :, :], w2_planes[:, PACK * c : PACK * (c + 1), :])
 
-        for step in range(N_STEPS):
+        def quantise_w2():
+            nc.vector.quantize_mx(
+                out=w2_codes[:].rearrange("p c n -> p (c n)").bitcast(FP8X4),
+                scales=w2_scales[:].rearrange("p c n -> p (c n)"),
+                in_=w2_grouped[:].rearrange("p c n t -> p (c n t)"),
+            )
+
+        columns = consts.tile([P, PACK + FEATURE_SLICES, 2 * PASSES], F32)
+
+        def turn_columns(tag):
+            columns_ps = bank([P, PACK + FEATURE_SLICES, P], tag, BF16)
+            for t in range(PACK):
+                nc.tensor.transpose(out=columns_ps[:, t, :], in_=affine_rows[:, t : t + PACK * (P - 1) + 1 : PACK], identity=ident_bf16[:])
+            for s in range(FEATURE_SLICES):
+                first = HIDDEN + s * P
+                nc.tensor.transpose(
+                    out=columns_ps[:, PACK + s, :], in_=bias_rows[:, first : first + P], identity=ident_bf16[:]
+                )
+            nc.vector.tensor_copy(out=columns[:], in_=columns_ps[:, :, 0 : 2 * PASSES])
+
+        transpose_x(0, 0)
+        regroup_w1(0, 0, 320)
+        copy_x(0, 0)
+        regroup_w1(1, 0, 320)
+        spread_bias(0, "h")
+        transpose_x(0, 1)
+        quantise_w1(0, 0)
+        copy_x(0, 1)
+        quantise_x_tile(0, 0)
+        quantise_w1(1, 0)
+        quantise_x_tile(0, 1)
+        spread_bias(BANK, "normedT")
+        layer1(0, 0, 0)
+        layer1(0, 1, 0)
+        transpose_x(1, 0)
+        transpose_x(1, 1)
+        regroup_w1(0, 1, 256)
+        add_b1(0, 0, 0)
+        regroup_w1(1, 1, 256)
+        copy_x(1, 0)
+        copy_x(1, 1)
+        transpose_x(2, 0, "x1")
+        transpose_x(2, 1, "pooled")
+        quantise_w1(0, 1)
+        quantise_w1(1, 1)
+        add_b1(0, 1, 0)
+        layer1(0, 0, 1, "normedT")
+        layer1(0, 1, 1, "normedT")
+        quantise_x(1)
+        copy_x(2, 0)
+        copy_x(2, 1)
+        for k in range(PAIR):
+            load_x(X_LOADS_AHEAD, k)
+        add_b1(0, 0, 1)
+        add_b1(0, 1, 1)
+        regroup_w2()
+
+        for step in range(1, RELU):
             for k in range(PAIR):
                 load_x(step + X_LOADS_AHEAD, k)
-            transpose_x(2 * (step + 1))
-            transpose_x(2 * (step + 1) + 1)
-            transpose_h(step - RELU, 0)
-            transpose_h(step - RELU, 1)
-            copy_x(2 * (step + 1))
-            copy_x(2 * (step + 1) + 1)
-            relu(step - RELU, 0)
-            relu(step - RELU, 1)
-            regroup_r(step - REGROUP, 0)
-            regroup_r(step - REGROUP, 1)
-            quantise_r(step - QUANT, 0)
-            quantise_r(step - QUANT, 1)
-            normalise(step - NORM)
-            square(step - 1, 0)
-            square(step - 1, 1)
+            spare = ("normedT", "normedT") if step == 1 else ("x1", "pooled")
             layer1(step, 0, 0)
             layer1(step, 0, 1)
-            repeat(step - REPEAT)
+            layer1(step, 1, 0, spare[0])
+            layer1(step, 1, 1, spare[1])
+            if step == 1:
+                transpose_x(3, 0)
+                transpose_x(3, 1)
+            add_b1(step, 0, 0)
+            mean(step - 1)
+            add_b1(step, 0, 1)
+            square(step - 1, 0)
+            square(step - 1, 1)
+            deviation(step - 1)
+            if step == 1:
+                copy_x(3, 0)
+                copy_x(3, 1)
+            normalise(step - NORM, on_vector=True)
+            quantise_x(step + 1)
+            add_b1(step, 1, 0)
+            add_b1(step, 1, 1)
+            if step == 1:
+                quantise_w2()
+                spread_bias(2 * BANK, "x1")
+                turn_columns("pooled")
+        mean(RELU - 1)
+        normalise(RELU - NORM)
+
+        for step in range(RELU, N_PAIRS):
+            for k in range(PAIR):
+                load_x(step + X_LOADS_AHEAD, k)
+            transpose_x(step + 1, 0)
+            transpose_x(step + 1, 1)
+            transpose_h(step - RELU, 0)
+            transpose_h(step - RELU, 1)
+            copy_x(step + 1, 0)
+            copy_x(step + 1, 1)
+            relu(step - RELU, 0)
+            relu(step - RELU, 1)
+            for c in range(PASSES):
+                regroup_r(step - REGROUP, c)
+            for c in range(PASSES):
+                quantise_r(step - REGROUP, c)
+            if step > RELU:
+                normalise(step - NORM)
+            square(step - 1, 0)
+            square(step - 1, 1)
+            for half in range(HALVES):
+                layer1(step, 0, half)
+                add_b1(step, 0, half)
+            layer2(step - LAYER2)
             transpose_x1(step - POOL)
             transpose_h(step - RELU, 2)
-            pool(step - POOL)
-            layer1(step, 1, 0)
-            layer1(step, 1, 1)
-            relu(step - RELU, 2)
-            layer2(step - LAYER2)
             transpose_h(step - RELU, 3)
+            pool(step - POOL)
+            add_b2(step - LAYER2)
+            for half in range(HALVES):
+                layer1(step, 1, half)
+                add_b1(step, 1, half)
+            relu(step - RELU, 2)
             relu(step - RELU, 3)
             quantise_x(step + 1)
-            evacuate_x1(step - X1_OUT)
             store_pooled(step - STORE)
+            repeat(step - POOL)
             deviation(step - 1)
             mean(step)
-            if step == 0:
-                spread_bias(2 * BANK)
-                load_affine()
-            if step == 1:
-                for c in range(PASSES):
-                    regroup(nc.vector.tensor_copy, w2_grouped[:, c, :, :], w2_planes[:, PACK * c : PACK * (c + 1), :])
-                nc.vector.quantize_mx(
-                    out=w2_codes[:].rearrange("p c n -> p (c n)").bitcast(FP8X4),
-                    scales=w2_scales[:].rearrange("p c n -> p (c n)"),
-                    in_=w2_grouped[:].rearrange("p c n t -> p (c n t)"),
-                )
+
+        last = N_PAIRS - 1
+
+        def transpose_all(p):
+            for u in range(UNITS):
+                transpose_h(p, u, "h" if u % 2 else "normedT")
+
+        store_pooled(last - 6)
+        transpose_all(last - 2)
+        for c in range(PASSES):
+            regroup_r(last - 3, c)
+        for c in range(PASSES):
+            quantise_r(last - 3, c)
+        layer2(last - 4)
+        for u in range(UNITS):
+            relu(last - 2, u)
+        transpose_x1(last - 5)
+        normalise(last - 1, on_vector=True)
+        add_b2(last - 4)
+        pool(last - 5)
+        for k in range(PAIR):
+            square(last, k)
+        deviation(last)
+        transpose_x1(last - 4, "xT")
+        layer2(last - 3, "xT")
+        transpose_all(last - 1)
+        for c in range(PASSES):
+            regroup_r(last - 2, c)
+        pool(last - 4)
+        add_b2(last - 3)
+        for c in range(PASSES):
+            quantise_r(last - 2, c)
+        relu(last - 1, 0)
+        relu(last - 1, 1)
+        repeat(last - 4)
+        relu(last - 1, 2)
+        relu(last - 1, 3)
+        transpose_x1(last - 3, "xT")
+        layer2(last - 2)
+        store_pooled(last - 4)
+        normalise(last, on_vector=True)
+        pool(last - 3)
+        add_b2(last - 2)
+        transpose_all(last)
+        transpose_x1(last - 2, "xT")
+        for c in range(PASSES):
+            regroup_r(last - 1, c)
+        quantise_r(last - 1, 0)
+        pool(last - 2)
+        quantise_r(last - 1, 1)
+        for u in range(UNITS):
+            relu(last, u)
+        repeat(last - 2)
+        layer2_transposed(last - 1, "xT")
+        layer2(last - 1)
+        store_pooled(last - 2)
+        for c in range(PASSES):
+            regroup_r(last, c)
+        pool(last - 1)
+        for c in range(PASSES):
+            quantise_r(last, c)
+        add_b2(last - 1)
+        layer2_transposed(last, "h")
+        layer2(last)
+        pool(last)
+        add_b2(last)
+        repeat(last, biased=False)
+        store_pooled(last, "h")

from contextlib import ExitStack

import concourse.mybir as mybir
from concourse.masks import make_identity

F32 = mybir.dt.float32
BF16 = mybir.dt.bfloat16
U32 = mybir.dt.uint32
U8 = mybir.dt.uint8
FP8X4 = mybir.dt.float8_e4m3fn_x4
ALU = mybir.AluOpType
ACT = mybir.ActivationFunctionType
AXIS = mybir.AxisListType

P = 128
PACK = 4
K_PASS = P * PACK
BANK = 512

TOKENS = 64 * 64
NODES = 64
HIDDEN = 1024
FEATURES = 256
PASSES = HIDDEN // K_PASS
SLICES = HIDDEN // P
EPS = 1e-5

FLOPS = 2 * TOKENS * HIDDEN * (HIDDEN + FEATURES)

PAIR = 2
PAIR_TOKENS = PAIR * P
N_PAIRS = TOKENS // PAIR_TOKENS
HALVES = HIDDEN // BANK
FEATURE_SLICES = FEATURES // P
UNITS = SLICES // 2

BATCH = 2
BATCH_LINES = BATCH * PAIR_TOKENS // NODES
COPIES = P // BATCH_LINES
BATCH_TOKENS = BATCH * PAIR_TOKENS

NORM = 2
RELU = 3
REGROUP = 4
LAYER2 = 5
POOL = 6
STORE = 7
X_LOADS_AHEAD = 4


def regroup(copy, grouped, planes):
    copy(
        out=grouped.rearrange("p (n i) t -> p n t i", i=4),
        in_=planes.rearrange("p t (n i) -> p n t i", i=4),
    )


def tile_sub_graph_pa_t_kernel(tc, x_nodes, w1, b1, gamma, beta, w2, b2, out):
    nc = tc.nc
    x_rows = x_nodes.flatten_outer_dims()
    out_rows = out.flatten_outer_dims()

    with ExitStack() as ctx:
        consts = ctx.enter_context(tc.tile_pool(name="consts", bufs=1))
        stage = ctx.enter_context(tc.tile_pool(name="stage", bufs=2))
        psum = ctx.enter_context(tc.psum_pool(name="psum", bufs=1))
        ctx.enter_context(tc.manual_schedule())

        bank_bufs = {"xT": 2, "h": 2, "normedT": 2, "x1": 1, "pooled": 1}

        def bank(shape, tag, dtype=F32):
            tile = psum.tile(shape, dtype, tag=tag, bufs=bank_bufs[tag])
            return tile

        x_tiles, x_banks, x_words, x_quantised = {}, {}, {}, {}
        h_banks, normed, row_sums, minus_mean, squared, inv_std = {}, {}, {}, {}, {}, {}
        normedT, r_planes, r_grouped, r_quantised = {}, {}, {}, {}
        x1_banks, x1_tiles, pooled_banks, line_max, repeated = {}, {}, {}, {}, {}

        def is_pair(p):
            return 0 <= p < N_PAIRS

        def load_x(p, k):
            if not is_pair(p):
                return
            if k == 0:
                x_pair = stage.tile([P, PAIR, HIDDEN], BF16, tag="x_sb", bufs=X_LOADS_AHEAD + 1)
                x_tiles[p] = x_pair
            first = p * PAIR_TOKENS + k * P
            nc.sync.dma_start(out=x_tiles[p][:, k, :], in_=x_rows[first : first + P, :])

        w1_passes = w1.rearrange("(c p t) n -> c p t n", c=PASSES, p=P, t=PACK)
        w1_planes = {}

        def load_w1(c, half):
            cols = slice(half * BANK, (half + 1) * BANK)
            planes = consts.tile([P, PACK, BANK], BF16, name="w1_planes_%d%d" % (c, half))
            nc.sync.dma_start(out=planes[:], in_=w1_passes[c][:, :, cols])
            w1_planes[c, half] = planes

        load_w1(0, 0)
        load_x(0, 0)

        bias_rows = consts.tile([P, HIDDEN + FEATURES], BF16)
        nc.vector.memset(bias_rows[:].bitcast(U32), 0)
        affine_rows = consts.tile([P, K_PASS], BF16)
        nc.vector.memset(affine_rows[:].bitcast(U32), 0)
        ones = consts.tile([P, P], BF16)
        nc.vector.memset(ones[:], 1.0)
        eps = consts.tile([P, 1], F32)
        nc.vector.memset(eps[:], EPS)
        warm = consts.tile([P, 1], F32)
        nc.scalar.activation(out=warm[:], in_=eps[:], func=ACT.Abs_reciprocal_sqrt)
        ident = consts.tile([P, P], F32)
        make_identity(nc, ident[:])
        ident_bf16 = consts.tile([P, P], BF16)
        nc.gpsimd.tensor_copy(out=ident_bf16[:], in_=ident[:])

        nc.sync.dma_start(out=bias_rows[0:1, 0:HIDDEN], in_=b1.rearrange("(o n) -> o n", o=1))
        load_w1(1, 0)
        load_x(0, 1)
        load_w1(0, 1)
        load_w1(1, 1)
        nc.sync.dma_start(out=bias_rows[0:1, HIDDEN:], in_=b2.rearrange("(o n) -> o n", o=1))
        nc.sync.dma_start(out=affine_rows[0:PASSES, :], in_=gamma.rearrange("(c n) -> c n", c=PASSES))
        nc.sync.dma_start(out=affine_rows[PASSES : 2 * PASSES, :], in_=beta.rearrange("(c n) -> c n", c=PASSES))
        for k in range(PAIR):
            load_x(1, k)
        w2_planes = consts.tile([P, PASSES * PACK, FEATURES], BF16)
        for c in range(PASSES):
            nc.sync.dma_start(
                out=w2_planes[:, PACK * c : PACK * (c + 1), :],
                in_=w2[c * K_PASS : (c + 1) * K_PASS, :].rearrange("(p t) n -> p t n", t=PACK),
            )
        for p in range(2, X_LOADS_AHEAD):
            for k in range(PAIR):
                load_x(p, k)

        def transpose_x(p, k, tag="xT"):
            if not is_pair(p):
                return
            words = x_tiles[p][:, k, :].bitcast(F32)
            xT_ps = bank([P, PASSES, 2, P], tag)
            for c in range(PASSES):
                for u in range(2):
                    nc.tensor.transpose(
                        out=xT_ps[:, c, u, :], in_=words[:, 2 * P * c + u : 2 * P * (c + 1) : 2], identity=ident[:]
                    )
            x_banks[p, k] = xT_ps

        def copy_x(p, k):
            if not is_pair(p):
                return
            if p == 0:
                words = stage.tile([P, PASSES, P, 2], F32, tag="x_grouped_first", bufs=2, align_bytes=64)
                x_words[p, k] = words[:]
            else:
                if k == 0:
                    x_pair = stage.tile([P, PAIR, PASSES, P, 2], F32, tag="x_grouped", bufs=2, align_bytes=64)
                    x_words[p] = x_pair
                x_words[p, k] = x_words[p][:, k]
            nc.scalar.copy(out=x_words[p, k], in_=x_banks[p, k][:].rearrange("q c u r -> q c r u"))

        def quantise_x_tile(p, k):
            x_codes = stage.tile([P, PASSES, P], U32, tag="x_codes_first", bufs=2, align_bytes=64)
            x_scales = stage.tile([P, PASSES, P], U8, tag="x_scales_first", bufs=2, align_bytes=64)
            nc.vector.quantize_mx(
                out=x_codes[:].rearrange("q c r -> q (c r)").bitcast(FP8X4),
                scales=x_scales[:].rearrange("q c r -> q (c r)"),
                in_=x_words[p, k].rearrange("q c r u -> q (c r u)").bitcast(BF16),
            )
            x_quantised[p, k] = (x_codes[:], x_scales[:])

        def quantise_x(p):
            if not is_pair(p):
                return
            x_codes = stage.tile([P, PAIR, PASSES, P], U32, tag="x_codes", bufs=2, align_bytes=64)
            x_scales = stage.tile([P, PAIR, PASSES, P], U8, tag="x_scales", bufs=2, align_bytes=64)
            nc.vector.quantize_mx(
                out=x_codes[:].rearrange("q k c r -> q (k c r)").bitcast(FP8X4),
                scales=x_scales[:].rearrange("q k c r -> q (k c r)"),
                in_=x_words[p][:].rearrange("q k c r u -> q (k c r u)").bitcast(BF16),
            )
            for k in range(PAIR):
                x_quantised[p, k] = (x_codes[:, k], x_scales[:, k])

        def layer1(p, k, half, tag="h"):
            if not is_pair(p):
                return
            x_codes, x_scales = x_quantised[p, k]
            cols = slice(half * BANK, (half + 1) * BANK)
            h_ps = bank([P, BANK], tag)
            for c in range(PASSES):
                nc.tensor.matmul_mx(
                    out=h_ps[:],
                    lhsT=x_codes[:, c, :].bitcast(FP8X4),
                    lhsT_scale=x_scales[:, c, :],
                    rhs=w1_codes[:, c, cols].bitcast(FP8X4),
                    rhs_scale=w1_scales[:, c, cols],
                    start=(c == 0),
                    stop=(c == PASSES - 1),
                )
            h_banks[p, k, half] = h_ps

        def add_b1(p, k, half):
            if not is_pair(p):
                return
            cols = slice(half * BANK, (half + 1) * BANK)
            if (p, k) not in normed:
                biased = stage.tile([P, HIDDEN], F32, tag="normed", bufs=16)
                normed[p, k] = biased
            if p not in row_sums:
                sums = stage.tile([P, HALVES, PAIR], F32, tag="sums", bufs=3)
                row_sums[p] = sums
            nc.vector.scalar_tensor_tensor(
                out=normed[p, k][:, cols].rearrange("r (t p) -> r t p", t=PACK),
                in0=h_banks[p, k, half][:].rearrange("r (p t) -> r t p", t=PACK),
                scalar=1.0,
                in1=b1_all[:, cols].rearrange("r (t p) -> r t p", t=PACK),
                op0=ALU.mult,
                op1=ALU.add,
                accum_out=row_sums[p][:, half, k : k + 1],
            )

        def mean(p):
            if not is_pair(p):
                return
            negated = stage.tile([P, PAIR], F32, tag="minus_mean", bufs=4)
            for k in range(PAIR):
                nc.vector.tensor_scalar(
                    out=negated[:, k : k + 1],
                    in0=row_sums[p][:, 0, k : k + 1],
                    scalar1=row_sums[p][:, 1, k : k + 1],
                    scalar2=-1.0 / HIDDEN,
                    op0=ALU.add,
                    op1=ALU.mult,
                )
            minus_mean[p] = negated

        def square(p, k):
            if not is_pair(p):
                return
            if p not in squared:
                sum_sq = stage.tile([P, PAIR], F32, tag="sum_sq", bufs=3)
                squared[p] = sum_sq
            squares = stage.tile([P, HIDDEN], BF16, tag="squares", bufs=2)
            nc.scalar.activation(
                out=squares[:],
                in_=normed[p, k][:],
                func=ACT.Square,
                bias=minus_mean[p][:, k : k + 1],
                scale=1.0,
                accum_out=squared[p][:, k : k + 1],
            )

        def deviation(p):
            if not is_pair(p):
                return
            inverse = stage.tile([P, PAIR], F32, tag="inv_std", bufs=3)
            nc.scalar.activation(
                out=inverse[:],
                in_=squared[p][:],
                func=ACT.Abs_reciprocal_sqrt,
                bias=eps[:, 0:1],
                scale=1.0 / HIDDEN,
            )
            inv_std[p] = inverse

        def normalise(p, on_vector=False):
            if not is_pair(p):
                return
            if on_vector:
                engine, factor = nc.vector, inv_std[p]
            else:
                gate = stage.tile([P, PAIR], F32, tag="gate", bufs=3)
                nc.vector.tensor_copy(out=gate[:], in_=inv_std[p][:])
                engine, factor = nc.gpsimd, gate
            for k in range(PAIR):
                engine.tensor_scalar(
                    out=normed[p, k][:],
                    in0=normed[p, k][:],
                    scalar1=minus_mean[p][:, k : k + 1],
                    scalar2=factor[:, k : k + 1],
                    op0=ALU.add,
                    op1=ALU.mult,
                )

        def transpose_h(p, u, tag="normedT"):
            if not is_pair(p):
                return
            normedT_ps = bank([P, 2, PAIR_TOKENS], tag)
            for v in range(2):
                s = 2 * u + v
                for k in range(PAIR):
                    nc.tensor.transpose(
                        out=normedT_ps[:, v, k * P : (k + 1) * P],
                        in_=normed[p, k][:, s * P : (s + 1) * P],
                        identity=ident[:],
                    )
            normedT[p, u] = normedT_ps

        def relu(p, u):
            if not is_pair(p):
                return
            if u == 0:
                planes = stage.tile([P, SLICES, PAIR_TOKENS], BF16, tag="r_planes", bufs=3)
                r_planes[p] = planes
            for v in range(2):
                s = 2 * u + v
                c, t = divmod(s, PACK)
                nc.scalar.activation(
                    out=r_planes[p][:, s, :],
                    in_=normedT[p, u][:, v, :],
                    func=ACT.Relu,
                    bias=columns[:, t, PASSES + c : PASSES + c + 1],
                    scale=columns[:, t, c : c + 1],
                )

        def regroup_r(p, c):
            if not is_pair(p):
                return
            grouped = stage.tile([P, PAIR_TOKENS, PACK], BF16, tag="r_grouped", bufs=4, align_bytes=64)
            regroup(nc.vector.tensor_copy, grouped[:], r_planes[p][:, PACK * c : PACK * (c + 1), :])
            r_grouped[p, c] = grouped

        def quantise_r(p, c):
            if not is_pair(p):
                return
            codes = stage.tile([P, PAIR_TOKENS], U32, tag="r_codes", bufs=6, align_bytes=64)
            scales = stage.tile([P, PAIR_TOKENS], U8, tag="r_scales", bufs=6, align_bytes=64)
            nc.vector.quantize_mx(
                out=codes[:].bitcast(FP8X4),
                scales=scales[:],
                in_=r_grouped[p, c][:].rearrange("p n t -> p (n t)"),
            )
            r_quantised[p, c] = (codes, scales)

        def layer2(p, tag="x1"):
            if not is_pair(p):
                return
            x1_ps = bank([P, PAIR, FEATURES], tag)
            for k in range(PAIR):
                for c in range(PASSES):
                    codes, scales = r_quantised[p, c]
                    nc.tensor.matmul_mx(
                        out=x1_ps[:, k, :],
                        lhsT=codes[:, k * P : (k + 1) * P].bitcast(FP8X4),
                        lhsT_scale=scales[:, k * P : (k + 1) * P],
                        rhs=w2_codes[:, c, :].bitcast(FP8X4),
                        rhs_scale=w2_scales[:, c, :],
                        start=(c == 0),
                        stop=(c == PASSES - 1),
                    )
            x1_banks[p] = x1_ps

        def add_b2(p):
            if not is_pair(p):
                return
            x1_sb = stage.tile([P, PAIR, FEATURES], F32, tag="x1_sb", bufs=5)
            nc.vector.tensor_tensor(
                out=x1_sb[:],
                in0=x1_banks[p][:],
                in1=b2_all.unsqueeze(1).to_broadcast([P, PAIR, FEATURES]),
                op=ALU.add,
            )
            x1_tiles[p] = x1_sb
            rows = slice(p * PAIR_TOKENS, (p + 1) * PAIR_TOKENS)
            nc.sync.dma_start(out=out_rows[rows, 0:FEATURES].rearrange("(k p) f -> p k f", p=P), in_=x1_sb[:])

        def transpose_x1(p, tag="pooled"):
            if not is_pair(p):
                return
            x1T_ps = bank([P, FEATURE_SLICES, PAIR_TOKENS], tag)
            for s in range(FEATURE_SLICES):
                for k in range(PAIR):
                    nc.tensor.transpose(
                        out=x1T_ps[:, s, k * P : (k + 1) * P],
                        in_=x1_tiles[p][:, k, s * P : (s + 1) * P],
                        identity=ident[:],
                    )
            pooled_banks[p] = x1T_ps

        def layer2_transposed(p, tag):
            x1T_ps = bank([P, FEATURE_SLICES, PAIR_TOKENS], tag)
            for s in range(FEATURE_SLICES):
                for c in range(PASSES):
                    codes, scales = r_quantised[p, c]
                    nc.tensor.matmul_mx(
                        out=x1T_ps[:, s, :],
                        lhsT=w2_codes[:, c, s * P : (s + 1) * P].bitcast(FP8X4),
                        lhsT_scale=w2_scales[:, c, s * P : (s + 1) * P],
                        rhs=codes[:].bitcast(FP8X4),
                        rhs_scale=scales[:],
                        start=(c == 0),
                        stop=(c == PASSES - 1),
                    )
            pooled_banks[p] = x1T_ps

        def pool(p):
            if not is_pair(p):
                return
            batch, member = divmod(p, BATCH)
            if member == 0:
                maxima = stage.tile([P, FEATURE_SLICES, BATCH_LINES], F32, tag="line_max", bufs=2)
                line_max[batch] = maxima
            lines = BATCH_LINES // BATCH
            nc.vector.tensor_reduce(
                out=line_max[batch][:, :, member * lines : (member + 1) * lines],
                in_=pooled_banks[p][:].rearrange("f s (b l) -> f s b l", l=NODES),
                axis=AXIS.X,
                op=ALU.max,
            )

        def repeat(p, biased=True):
            if not is_pair(p) or p % BATCH != BATCH - 1:
                return
            batch = p // BATCH
            copies = stage.tile([P, FEATURE_SLICES, BATCH_LINES, COPIES], F32, tag="repeated", bufs=2)
            if biased:
                nc.scalar.copy(
                    out=copies[:],
                    in_=line_max[batch][:].unsqueeze(3).to_broadcast([P, FEATURE_SLICES, BATCH_LINES, COPIES]),
                )
            else:
                for s in range(FEATURE_SLICES):
                    nc.scalar.activation(
                        out=copies[:, s],
                        in_=line_max[batch][:, s].unsqueeze(2).to_broadcast([P, BATCH_LINES, COPIES]),
                        func=ACT.Identity,
                        bias=columns[:, PACK + s, 0:1],
                        scale=1.0,
                    )
            repeated[batch] = copies

        def store_pooled(p, tag="pooled"):
            if not is_pair(p) or p % BATCH != BATCH - 1:
                return
            batch = p // BATCH
            x2_ps = bank([P, FEATURES], tag)
            for s in range(FEATURE_SLICES):
                nc.tensor.transpose(
                    out=x2_ps[:, s * P : (s + 1) * P],
                    in_=repeated[batch][:, s, :, :].rearrange("f b i -> f (b i)"),
                    identity=ident[:],
                )
            x2_sb = stage.tile([P, FEATURES], F32, tag="x2_sb", bufs=2)
            nc.scalar.copy(out=x2_sb[:], in_=x2_ps[:])
            rows = slice(batch * BATCH_TOKENS, (batch + 1) * BATCH_TOKENS)
            nodes_each = NODES // COPIES
            nc.sync.dma_start(
                out=out_rows[rows, FEATURES : 2 * FEATURES].rearrange("(p m) f -> p m f", m=nodes_each),
                in_=x2_sb[:].unsqueeze(1).to_broadcast([P, nodes_each, FEATURES]),
            )

        bias_all = consts.tile([P, HIDDEN + FEATURES], BF16)
        b1_all = bias_all[:, 0:HIDDEN]
        b2_all = bias_all[:, HIDDEN:]

        def spread_bias(first, tag):
            width = min(BANK, HIDDEN + FEATURES - first)
            bias_ps = bank([P, BANK], tag)
            nc.tensor.matmul(
                out=bias_ps[:, 0:width],
                lhsT=ones[:],
                rhs=bias_rows[:, first : first + width],
                start=True,
                stop=True,
            )
            if first < HIDDEN:
                nc.scalar.copy(
                    out=bias_all[:, first : first + width].rearrange("r (t p) -> r t p", t=PACK),
                    in_=bias_ps[:].rearrange("r (p t) -> r t p", t=PACK),
                )
            else:
                nc.scalar.copy(out=bias_all[:, first : first + width], in_=bias_ps[:, 0:width])

        w1_codes = consts.tile([P, PASSES, HIDDEN], U32, align_bytes=64)
        w1_scales = consts.tile([P, PASSES, HIDDEN], U8, align_bytes=64)
        w1_grouped = {}

        def regroup_w1(c, half, on_vector):
            grouped = stage.tile([P, BANK, PACK], BF16, tag="w1_grouped", bufs=2, align_bytes=64)
            planes = w1_planes[c, half]
            regroup(nc.vector.tensor_copy, grouped[:, 0:on_vector, :], planes[:, :, 0:on_vector])
            regroup(nc.scalar.copy, grouped[:, on_vector:BANK, :], planes[:, :, on_vector:BANK])
            w1_grouped[c, half] = grouped

        def quantise_w1(c, half):
            cols = slice(half * BANK, (half + 1) * BANK)
            nc.vector.quantize_mx(
                out=w1_codes[:, c, cols].bitcast(FP8X4),
                scales=w1_scales[:, c, cols],
                in_=w1_grouped[c, half][:].rearrange("p n t -> p (n t)"),
            )

        w2_grouped = consts.tile([P, PASSES, FEATURES, PACK], BF16, align_bytes=64)
        w2_codes = consts.tile([P, PASSES, FEATURES], U32, align_bytes=64)
        w2_scales = consts.tile([P, PASSES, FEATURES], U8, align_bytes=64)

        def regroup_w2():
            for c in range(PASSES):
                regroup(nc.scalar.copy, w2_grouped[:, c, :, :], w2_planes[:, PACK * c : PACK * (c + 1), :])

        def quantise_w2():
            nc.vector.quantize_mx(
                out=w2_codes[:].rearrange("p c n -> p (c n)").bitcast(FP8X4),
                scales=w2_scales[:].rearrange("p c n -> p (c n)"),
                in_=w2_grouped[:].rearrange("p c n t -> p (c n t)"),
            )

        columns = consts.tile([P, PACK + FEATURE_SLICES, 2 * PASSES], F32)

        def turn_columns(tag):
            columns_ps = bank([P, PACK + FEATURE_SLICES, P], tag, BF16)
            for t in range(PACK):
                nc.tensor.transpose(out=columns_ps[:, t, :], in_=affine_rows[:, t : t + PACK * (P - 1) + 1 : PACK], identity=ident_bf16[:])
            for s in range(FEATURE_SLICES):
                first = HIDDEN + s * P
                nc.tensor.transpose(
                    out=columns_ps[:, PACK + s, :], in_=bias_rows[:, first : first + P], identity=ident_bf16[:]
                )
            nc.vector.tensor_copy(out=columns[:], in_=columns_ps[:, :, 0 : 2 * PASSES])

        transpose_x(0, 0)
        regroup_w1(0, 0, 320)
        copy_x(0, 0)
        regroup_w1(1, 0, 320)
        spread_bias(0, "h")
        transpose_x(0, 1)
        quantise_w1(0, 0)
        copy_x(0, 1)
        quantise_x_tile(0, 0)
        quantise_w1(1, 0)
        quantise_x_tile(0, 1)
        spread_bias(BANK, "normedT")
        layer1(0, 0, 0)
        layer1(0, 1, 0)
        transpose_x(1, 0)
        transpose_x(1, 1)
        regroup_w1(0, 1, 256)
        add_b1(0, 0, 0)
        regroup_w1(1, 1, 256)
        copy_x(1, 0)
        copy_x(1, 1)
        transpose_x(2, 0, "x1")
        transpose_x(2, 1, "pooled")
        quantise_w1(0, 1)
        quantise_w1(1, 1)
        add_b1(0, 1, 0)
        layer1(0, 0, 1, "normedT")
        layer1(0, 1, 1, "normedT")
        quantise_x(1)
        copy_x(2, 0)
        copy_x(2, 1)
        for k in range(PAIR):
            load_x(X_LOADS_AHEAD, k)
        add_b1(0, 0, 1)
        add_b1(0, 1, 1)
        regroup_w2()

        for step in range(1, RELU):
            for k in range(PAIR):
                load_x(step + X_LOADS_AHEAD, k)
            spare = ("normedT", "normedT") if step == 1 else ("x1", "pooled")
            layer1(step, 0, 0)
            layer1(step, 0, 1)
            layer1(step, 1, 0, spare[0])
            layer1(step, 1, 1, spare[1])
            if step == 1:
                transpose_x(3, 0)
                transpose_x(3, 1)
            add_b1(step, 0, 0)
            mean(step - 1)
            add_b1(step, 0, 1)
            square(step - 1, 0)
            square(step - 1, 1)
            deviation(step - 1)
            if step == 1:
                copy_x(3, 0)
                copy_x(3, 1)
            normalise(step - NORM, on_vector=True)
            quantise_x(step + 1)
            add_b1(step, 1, 0)
            add_b1(step, 1, 1)
            if step == 1:
                quantise_w2()
                spread_bias(2 * BANK, "x1")
                turn_columns("pooled")
        mean(RELU - 1)
        normalise(RELU - NORM)

        for step in range(RELU, N_PAIRS):
            for k in range(PAIR):
                load_x(step + X_LOADS_AHEAD, k)
            transpose_x(step + 1, 0)
            transpose_x(step + 1, 1)
            transpose_h(step - RELU, 0)
            transpose_h(step - RELU, 1)
            copy_x(step + 1, 0)
            copy_x(step + 1, 1)
            relu(step - RELU, 0)
            relu(step - RELU, 1)
            for c in range(PASSES):
                regroup_r(step - REGROUP, c)
            for c in range(PASSES):
                quantise_r(step - REGROUP, c)
            if step > RELU:
                normalise(step - NORM)
            square(step - 1, 0)
            square(step - 1, 1)
            for half in range(HALVES):
                layer1(step, 0, half)
                add_b1(step, 0, half)
            layer2(step - LAYER2)
            transpose_x1(step - POOL)
            transpose_h(step - RELU, 2)
            transpose_h(step - RELU, 3)
            pool(step - POOL)
            add_b2(step - LAYER2)
            for half in range(HALVES):
                layer1(step, 1, half)
                add_b1(step, 1, half)
            relu(step - RELU, 2)
            relu(step - RELU, 3)
            quantise_x(step + 1)
            store_pooled(step - STORE)
            repeat(step - POOL)
            deviation(step - 1)
            mean(step)

        last = N_PAIRS - 1

        def transpose_all(p):
            for u in range(UNITS):
                transpose_h(p, u, "h" if u % 2 else "normedT")

        store_pooled(last - 6)
        transpose_all(last - 2)
        for c in range(PASSES):
            regroup_r(last - 3, c)
        for c in range(PASSES):
            quantise_r(last - 3, c)
        layer2(last - 4)
        for u in range(UNITS):
            relu(last - 2, u)
        transpose_x1(last - 5)
        normalise(last - 1, on_vector=True)
        add_b2(last - 4)
        pool(last - 5)
        for k in range(PAIR):
            square(last, k)
        deviation(last)
        transpose_x1(last - 4, "xT")
        layer2(last - 3, "xT")
        transpose_all(last - 1)
        for c in range(PASSES):
            regroup_r(last - 2, c)
        pool(last - 4)
        add_b2(last - 3)
        for c in range(PASSES):
            quantise_r(last - 2, c)
        relu(last - 1, 0)
        relu(last - 1, 1)
        repeat(last - 4)
        relu(last - 1, 2)
        relu(last - 1, 3)
        transpose_x1(last - 3, "xT")
        layer2(last - 2)
        store_pooled(last - 4)
        normalise(last, on_vector=True)
        pool(last - 3)
        add_b2(last - 2)
        transpose_all(last)
        transpose_x1(last - 2, "xT")
        for c in range(PASSES):
            regroup_r(last - 1, c)
        quantise_r(last - 1, 0)
        pool(last - 2)
        quantise_r(last - 1, 1)
        for u in range(UNITS):
            relu(last, u)
        repeat(last - 2)
        layer2_transposed(last - 1, "xT")
        layer2(last - 1)
        store_pooled(last - 2)
        for c in range(PASSES):
            regroup_r(last, c)
        pool(last - 1)
        for c in range(PASSES):
            quantise_r(last, c)
        add_b2(last - 1)
        layer2_transposed(last, "h")
        layer2(last)
        pool(last)
        add_b2(last)
        repeat(last, biased=False)
        store_pooled(last, "h")
